import numpy as np
import ml_dtypes


def mxq(x, axis, fmt="e4m3"):
    dtype, down = {"e4m3": (ml_dtypes.float8_e4m3fn, 7), "e5m2": (ml_dtypes.float8_e5m2, 14)}[fmt]
    v = np.moveaxis(np.asarray(x, np.float32).astype(ml_dtypes.bfloat16).astype(np.float64), axis, -1)
    blocks = v.reshape(v.shape[:-1] + (-1, 32))
    amax = np.abs(blocks).max(-1, keepdims=True)
    byte = np.maximum(np.where(amax > 0, np.frexp(amax)[1] - 1 + 127, 0) - down, 1)
    scale = np.exp2(byte - 127.0)
    codes = (blocks / scale).astype(np.float32).astype(dtype).astype(np.float64)
    return np.moveaxis((codes * scale).reshape(v.shape), -1, axis)


WIDE = False


def mx_kscale(k):
    if not WIDE:
        return np.ones(k)
    levels = np.array([10, -10, 5, -5, 0])
    a = np.random.permutation(np.resize(levels, k // 512 * 4)).reshape(k // 512, 4)
    idx = np.arange(k)
    return np.exp2(a[idx // 512, idx % 128 // 32])


BF16 = ml_dtypes.bfloat16


def bf(x):
    return np.asarray(x, np.float32).astype(BF16)


def f64(x):
    return np.asarray(x).astype(np.float64)


B, C_IN, H, W, D, P, NC = 16, 512, 16, 16, 512, 2048, 256
HW = H * W


def sigmoid(v):
    return 1.0 / (1.0 + np.exp(-v))


def setup_inputs():
    s = mx_kscale(D)
    return {"h_relu": bf(np.maximum(np.random.standard_normal((B, D, H, W)) * np.sqrt(2.0), 0.0) * s[None, :, None, None]),
            "conv2_w": bf(np.random.standard_normal((D, D)) * np.sqrt(2.0 / D) / s[None, :]),
            "conv2_b": bf(np.random.standard_normal(D) * 0.5),
            "prototypes": bf(np.random.uniform(size=(P, D)))}


def reference(h_relu, conv2_w, conv2_b, prototypes):
    h = f64(h_relu).reshape(B, D, HW)
    z = (mxq(f64(conv2_w), 1, "e4m3") @ mxq(h, 1, "e4m3")) + f64(conv2_b)[None, :, None]
    f = sigmoid(z)
    pr = f64(prototypes)
    f2 = np.sum(f * f, axis=1)
    p2 = np.sum(pr * pr, axis=1)
    fp = mxq(pr, 1, "e4m3") @ mxq(f, 1, "e4m3")
    distances = f2[:, None, :] + p2[None, :, None] - 2.0 * fp
    return np.min(distances, axis=-1)

@@ -1,0 +1,280 @@
+from contextlib import ExitStack
+
+import concourse.mybir as mybir
+from concourse.masks import make_identity
+
+F32 = mybir.dt.float32
+BF16 = mybir.dt.bfloat16
+U32 = mybir.dt.uint32
+U8 = mybir.dt.uint8
+FP8X4 = mybir.dt.float8_e4m3fn_x4
+ACT = mybir.ActivationFunctionType
+ALU = mybir.AluOpType
+AX = mybir.AxisListType
+
+P = 128
+NIMG = 16
+HW = 256
+CH = 512
+NPROTO = 2048
+GI = 4
+NG = NIMG // GI
+RPOS = P // GI
+NJ = HW // RPOS
+CW = 512
+NCHUNK = NIMG * HW // CW
+NPC = NPROTO // 512
+
+FLOPS = 2 * CH * CH * NIMG * HW + 2 * NPROTO * CH * NIMG * HW
+MANUAL = True
+
+
+def tile_protopnet_pa_kernel(tc, h_relu, conv2_w, conv2_b, prototypes, out):
+    nc = tc.nc
+    with ExitStack() as ctx:
+        if MANUAL:
+            ctx.enter_context(tc.manual_schedule())
+        const = ctx.enter_context(tc.tile_pool(name="const", bufs=1))
+        work = ctx.enter_context(tc.tile_pool(name="work", bufs=2))
+        psum = ctx.enter_context(tc.psum_pool(name="psum", bufs=2))
+
+        w_sb = const.tile([P, 4, CH], BF16)
+        nc.sync.dma_start(out=w_sb[:], in_=conv2_w.rearrange("(q t) c -> q t c", t=4))
+        b_bf = const.tile([P, 4], BF16)
+        nc.scalar.dma_start(out=b_bf[:], in_=conv2_b.rearrange("(q t) -> q t", t=4))
+        h_sb = [None] * NG
+        proto_sb = const.tile([P, 16, CH], BF16)
+
+        def load_h(g):
+            h_sb[g] = work.tile([P, GI, 4 * HW], BF16, name="h_sb", bufs=NG)
+            nc.sync.dma_start(
+                out=h_sb[g][:],
+                in_=h_relu[g * GI:(g + 1) * GI].rearrange("i (p j) y x -> p i (j y x)", j=4),
+            )
+
+        def load_proto(pc):
+            nc.sync.dma_start(
+                out=proto_sb[:, 4 * pc:4 * pc + 4, :],
+                in_=prototypes[pc * 512:(pc + 1) * 512, :].rearrange("(a r) d -> r a d", r=P),
+            )
+
+        load_h(0)
+        load_proto(0)
+        load_proto(1)
+        load_h(1)
+        load_proto(2)
+        load_proto(3)
+        load_h(2)
+        load_h(3)
+
+        ident = const.tile([P, P], F32)
+        make_identity(nc, ident[:])
+        neghalf = const.tile([P, 2], F32)
+        nc.vector.memset(neghalf[:], -0.5)
+        b_f32 = const.tile([P, 4], F32)
+        nc.vector.tensor_copy(out=b_f32[:], in_=b_bf[:])
+
+        wcodes = const.tile([P, CH], U32, align_bytes=64)
+        wscales = const.tile([P, CH], U8, align_bytes=64)
+        pcodes = const.tile([P, NPROTO], U32, align_bytes=64)
+        pscales = const.tile([P, NPROTO], U8, align_bytes=64)
+        p2_sb = const.tile([P, 16], F32)
+        junk = const.tile([P, CH], BF16)
+        best = const.tile([P, NIMG * 16], F32)
+
+        def words_to_mx(src, first_tile, codes, scales, evac):
+            grouped = work.tile([P, 4 * 512], BF16, name="grouped", align_bytes=64)
+            gw = grouped[:].bitcast(F32)
+            for half in range(2):
+                bank = psum.tile([P, 2, 2, P], F32, name="tp")
+                for a in range(2):
+                    words = src[:, first_tile + 2 * half + a, :].bitcast(F32)
+                    words = words.rearrange("r (q u) -> r u q", u=2)
+                    for u in range(2):
+                        nc.tensor.transpose(bank[:, a, u, :], words[:, u, :], ident[:])
+                evac(
+                    gw[:, half * 512:(half + 1) * 512].rearrange("q (a r u) -> q a r u", a=2, u=2),
+                    bank[:].rearrange("q a u r -> q a r u"),
+                )
+            nc.vector.quantize_mx(out=codes.bitcast(FP8X4), scales=scales, in_=grouped[:])
+
+        def evac_s(o, i):
+            nc.scalar.copy(out=o, in_=i)
+
+        def evac_v(o, i):
+            nc.vector.tensor_copy(out=o, in_=i)
+
+        hg = [None] * NG
+        hcodes = [None] * NCHUNK
+        hscales = [None] * NCHUNK
+        f32c = [None] * NCHUNK
+        sqc = [None] * NCHUNK
+        fgc = [None] * NCHUNK
+        fcodes = [None] * NCHUNK
+        fscales = [None] * NCHUNK
+        ng_sb = [None] * NCHUNK
+        rmax = [None] * NPC
+
+        def hreg(g, eng, j0=0, j1=NJ):
+            if hg[g] is None:
+                hg[g] = work.tile([P, GI * HW * 4], BF16, name="hg", align_bytes=64)
+            dst = hg[g][:].rearrange("p (j i r c) -> p i j r c", j=NJ, i=GI, c=4)
+            for i in range(GI):
+                src = h_sb[g][:, i, :].rearrange("p (c j r) -> p j r c", c=4, j=NJ)
+                if eng == "v":
+                    nc.vector.tensor_copy(out=dst[:, i, j0:j1], in_=src[:, j0:j1])
+                else:
+                    nc.gpsimd.tensor_scalar(out=dst[:, i, j0:j1], in0=src[:, j0:j1], scalar1=1.0,
+                                            scalar2=0.0, op0=ALU.mult, op1=ALU.add)
+
+        def quant_h(m):
+            hcodes[m] = work.tile([P, CW], U32, name="hcodes", bufs=4, align_bytes=64)
+            hscales[m] = work.tile([P, CW], U8, name="hscales", bufs=4, align_bytes=64)
+            half = m % 2
+            nc.vector.quantize_mx(out=hcodes[m][:].bitcast(FP8X4), scales=hscales[m][:],
+                                  in_=hg[m // 2][:, half * 4 * CW:(half + 1) * 4 * CW])
+
+        def st1(m, t):
+            if t == 0:
+                f32c[m] = work.tile([P, 4, CW], F32, name="f32c", bufs=3)
+            z = psum.tile([P, CW], F32, name="z")
+            nc.tensor.matmul_mx(out=z[:], lhsT=wcodes[:, t * P:(t + 1) * P].bitcast(FP8X4),
+                                lhsT_scale=wscales[:, t * P:(t + 1) * P],
+                                rhs=hcodes[m][:].bitcast(FP8X4), rhs_scale=hscales[m][:],
+                                start=True, stop=True)
+            nc.scalar.activation(out=f32c[m][:, t, :], in_=z[:], func=ACT.Sigmoid,
+                                 bias=b_f32[:, t:t + 1], scale=1.0)
+
+        def square(m):
+            sqc[m] = work.tile([P, 4, CW], F32, name="sqc")
+            nc.scalar.activation(out=sqc[m][:], in_=f32c[m][:], func=ACT.Square)
+
+        def fint(m, eng):
+            fgc[m] = work.tile([P, 4 * CW], BF16, name="fgc", align_bytes=64)
+            dst = fgc[m][:].rearrange("p (c t) -> p c t", t=4)
+            src = f32c[m][:].rearrange("p t c -> p c t")
+            if eng == "v":
+                nc.vector.tensor_copy(out=dst, in_=src)
+            else:
+                nc.gpsimd.tensor_scalar(out=dst, in0=src, scalar1=1.0, scalar2=0.0,
+                                        op0=ALU.mult, op1=ALU.add)
+
+        def quant_f(m):
+            fcodes[m] = work.tile([P, CW], U32, name="fcodes", bufs=4, align_bytes=64)
+            fscales[m] = work.tile([P, CW], U8, name="fscales", bufs=4, align_bytes=64)
+            nc.vector.quantize_mx(out=fcodes[m][:].bitcast(FP8X4), scales=fscales[m][:], in_=fgc[m][:])
+
+        def ngmm(m):
+            ngp = psum.tile([P, 4, 2], F32, name="ngp", bufs=1)
+            for jl in range(4):
+                for t in range(4):
+                    nc.tensor.matmul(out=ngp[:, jl, :], lhsT=sqc[m][:, t, jl * P:(jl + 1) * P],
+                                     rhs=neghalf[:], start=(t == 0), stop=(t == 3))
+            ng_sb[m] = work.tile([P, 4, 2], F32, name="ng_sb", bufs=4)
+            nc.scalar.copy(out=ng_sb[m][:], in_=ngp[:])
+
+        def st2(g, j):
+            m = 2 * g + j // 4
+            jl = j % 4
+            for pc in range(NPC):
+                x = psum.tile([P, 512], F32, name="x", bufs=3)
+                nc.tensor.matmul_mx(out=x[:], lhsT=fcodes[m][:, jl * P:(jl + 1) * P].bitcast(FP8X4),
+                                    lhsT_scale=fscales[m][:, jl * P:(jl + 1) * P],
+                                    rhs=pcodes[:, pc * 512:(pc + 1) * 512].bitcast(FP8X4),
+                                    rhs_scale=pscales[:, pc * 512:(pc + 1) * 512],
+                                    start=True, stop=True)
+                if j == 0:
+                    rmax[pc] = work.tile([P, 512], F32, name="rmax%d" % pc)
+                    nc.scalar.activation(out=rmax[pc][:], in_=x[:], func=ACT.Identity,
+                                         bias=ng_sb[m][:, jl, 0:1], scale=1.0)
+                else:
+                    nc.vector.scalar_tensor_tensor(out=rmax[pc][:], in0=x[:], scalar=ng_sb[m][:, jl, 0:1],
+                                                   in1=rmax[pc][:], op0=ALU.add, op1=ALU.max)
+
+        def fold_partitions(g, tiles):
+            bview = best[:].rearrange("p (b t) -> p t b", t=16)
+            for pc in range(NPC):
+                bank = psum.tile([P, 4, P], F32, name="tp")
+                for a in range(4):
+                    nc.tensor.transpose(bank[:, a, :], tiles[pc][:, a * P:(a + 1) * P], ident[:])
+                nc.vector.tensor_reduce(out=bview[:, 4 * pc:4 * pc + 4, GI * g:GI * (g + 1)],
+                                        in_=bank[:].rearrange("p a (i r) -> p a i r", i=GI),
+                                        axis=AX.X, op=ALU.max)
+
+        def p2_part(rt):
+            nc.scalar.activation(out=junk[:], in_=proto_sb[:, rt, :], func=ACT.Square,
+                                 accum_out=p2_sb[:, rt:rt + 1])
+
+        words_to_mx(w_sb, 0, wcodes[:], wscales[:], evac_s)
+        hreg(0, "v", 0, 4)
+        quant_h(0)
+        hreg(0, "v", 4, 8)
+        quant_h(1)
+        for t in range(4):
+            st1(0, t)
+        words_to_mx(proto_sb, 0, pcodes[:, 0:512], pscales[:, 0:512], evac_v)
+        fint(0, "g")
+        hreg(1, "g", 0, 4)
+        hreg(1, "g", 4, 8)
+        square(0)
+        words_to_mx(proto_sb, 4, pcodes[:, 512:1024], pscales[:, 512:1024], evac_v)
+        quant_f(0)
+        words_to_mx(proto_sb, 8, pcodes[:, 1024:1536], pscales[:, 1024:1536], evac_s)
+        words_to_mx(proto_sb, 12, pcodes[:, 1536:2048], pscales[:, 1536:2048], evac_s)
+        ngmm(0)
+
+        old = list(rmax)
+        for k in range(NCHUNK):
+            g = k // 2
+            for s in range(4):
+                j = 4 * (k % 2) + s
+                if j == 0:
+                    old = list(rmax)
+                st2(g, j)
+                if j == 0 and g > 0:
+                    fold_partitions(g - 1, old)
+                if k == 0 and s == 0:
+                    for t in range(4):
+                        st1(1, t)
+                if k == 0:
+                    if s >= 2:
+                        st1(2, 2 * s - 4)
+                        st1(2, 2 * s - 3)
+                elif k + 2 < NCHUNK:
+                    st1(k + 2, s)
+                if k + 1 < NCHUNK:
+                    if s == 0:
+                        square(k + 1)
+                        fint(k + 1, "g")
+                    if s == 2:
+                        ngmm(k + 1)
+                        quant_f(k + 1)
+                if k == 0:
+                    if s == 1:
+                        quant_h(2)
+                    if s == 3:
+                        quant_h(3)
+                elif s == 1 and k + 3 < NCHUNK:
+                    quant_h(k + 3)
+                if s == 1 and k % 2 == 0 and g + 2 < NG:
+                    hreg(g + 2, "g")
+                if s == 3:
+                    p2_part(2 * k)
+                    p2_part(2 * k + 1)
+        fold_partitions(NG - 1, rmax)
+
+        res = const.tile([P, NIMG * 16], F32)
+        nc.vector.scalar_tensor_tensor(
+            out=res[:].rearrange("p (b t) -> p b t", t=16),
+            in0=best[:].rearrange("p (b t) -> p b t", t=16),
+            scalar=-2.0,
+            in1=p2_sb[:].unsqueeze(1).to_broadcast([P, NIMG, 16]),
+            op0=ALU.mult, op1=ALU.add)
+        tpf = psum.tile([P, 2, P], F32, name="tp")
+        for hb in range(2):
+            nc.tensor.transpose(tpf[:, hb, :], res[:, hb * P:(hb + 1) * P], ident[:])
+        o_sb = const.tile([P, 2, P], F32)
+        nc.vector.tensor_copy(out=o_sb[:], in_=tpf[:])
+        nc.sync.dma_start(
+            out=out.rearrange("b (t p) -> (b t) p", p=P).rearrange("(h c) p -> c h p", h=2),
+            in_=o_sb[:])

@@ -26,7 +26,7 @@ NCHUNK = NIMG * HW // CW
 NPC = NPROTO // 512
 
 FLOPS = 2 * CH * CH * NIMG * HW + 2 * NPROTO * CH * NIMG * HW
-MANUAL = True
+MANUAL = False
 
 
 def tile_protopnet_pa_kernel(tc, h_relu, conv2_w, conv2_b, prototypes, out):
@@ -69,8 +69,6 @@ def tile_protopnet_pa_kernel(tc, h_relu, conv2_w, conv2_b, prototypes, out):
 
         ident = const.tile([P, P], F32)
         make_identity(nc, ident[:])
-        neghalf = const.tile([P, 2], F32)
-        nc.vector.memset(neghalf[:], -0.5)
         b_f32 = const.tile([P, 4], F32)
         nc.vector.tensor_copy(out=b_f32[:], in_=b_bf[:])
 
@@ -80,6 +78,7 @@ def tile_protopnet_pa_kernel(tc, h_relu, conv2_w, conv2_b, prototypes, out):
         pscales = const.tile([P, NPROTO], U8, align_bytes=64)
         p2_sb = const.tile([P, 16], F32)
         junk = const.tile([P, CH], BF16)
+        junk32 = const.tile([P, CH], BF16)
         best = const.tile([P, NIMG * 16], F32)
 
         def words_to_mx(src, first_tile, codes, scales, evac):
@@ -108,7 +107,7 @@ def tile_protopnet_pa_kernel(tc, h_relu, conv2_w, conv2_b, prototypes, out):
         hcodes = [None] * NCHUNK
         hscales = [None] * NCHUNK
         f32c = [None] * NCHUNK
-        sqc = [None] * NCHUNK
+        f2c = [None] * NCHUNK
         fgc = [None] * NCHUNK
         fcodes = [None] * NCHUNK
         fscales = [None] * NCHUNK
@@ -145,9 +144,18 @@ def tile_protopnet_pa_kernel(tc, h_relu, conv2_w, conv2_b, prototypes, out):
             nc.scalar.activation(out=f32c[m][:, t, :], in_=z[:], func=ACT.Sigmoid,
                                  bias=b_f32[:, t:t + 1], scale=1.0)
 
-        def square(m):
-            sqc[m] = work.tile([P, 4, CW], F32, name="sqc")
-            nc.scalar.activation(out=sqc[m][:], in_=f32c[m][:], func=ACT.Square)
+        def f2_tile(m, jl):
+            if jl == 0:
+                f2c[m] = work.tile([P, 4], F32, name="f2c", bufs=4)
+            bank = psum.tile([P, 4, P], F32, name="tp")
+            for t in range(4):
+                nc.tensor.transpose(bank[:, t, :], f32c[m][:, t, jl * P:(jl + 1) * P], ident[:])
+            nc.scalar.activation(out=junk32[:], in_=bank[:].rearrange("p t q -> p (t q)"), func=ACT.Square,
+                                 accum_out=f2c[m][:, jl:jl + 1])
+
+        def ngscale(m):
+            ng_sb[m] = work.tile([P, 4], F32, name="ng_sb", bufs=4)
+            nc.scalar.mul(out=ng_sb[m][:], in_=f2c[m][:], mul=-0.5)
 
         def fint(m, eng):
             fgc[m] = work.tile([P, 4 * CW], BF16, name="fgc", align_bytes=64)
@@ -164,20 +172,11 @@ def tile_protopnet_pa_kernel(tc, h_relu, conv2_w, conv2_b, prototypes, out):
             fscales[m] = work.tile([P, CW], U8, name="fscales", bufs=4, align_bytes=64)
             nc.vector.quantize_mx(out=fcodes[m][:].bitcast(FP8X4), scales=fscales[m][:], in_=fgc[m][:])
 
-        def ngmm(m):
-            ngp = psum.tile([P, 4, 2], F32, name="ngp", bufs=1)
-            for jl in range(4):
-                for t in range(4):
-                    nc.tensor.matmul(out=ngp[:, jl, :], lhsT=sqc[m][:, t, jl * P:(jl + 1) * P],
-                                     rhs=neghalf[:], start=(t == 0), stop=(t == 3))
-            ng_sb[m] = work.tile([P, 4, 2], F32, name="ng_sb", bufs=4)
-            nc.scalar.copy(out=ng_sb[m][:], in_=ngp[:])
-
         def st2(g, j):
             m = 2 * g + j // 4
             jl = j % 4
             for pc in range(NPC):
-                x = psum.tile([P, 512], F32, name="x", bufs=3)
+                x = psum.tile([P, 512], F32, name="x", bufs=4)
                 nc.tensor.matmul_mx(out=x[:], lhsT=fcodes[m][:, jl * P:(jl + 1) * P].bitcast(FP8X4),
                                     lhsT_scale=fscales[m][:, jl * P:(jl + 1) * P],
                                     rhs=pcodes[:, pc * 512:(pc + 1) * 512].bitcast(FP8X4),
@@ -186,20 +185,19 @@ def tile_protopnet_pa_kernel(tc, h_relu, conv2_w, conv2_b, prototypes, out):
                 if j == 0:
                     rmax[pc] = work.tile([P, 512], F32, name="rmax%d" % pc)
                     nc.scalar.activation(out=rmax[pc][:], in_=x[:], func=ACT.Identity,
-                                         bias=ng_sb[m][:, jl, 0:1], scale=1.0)
+                                         bias=ng_sb[m][:, jl:jl + 1], scale=1.0)
                 else:
-                    nc.vector.scalar_tensor_tensor(out=rmax[pc][:], in0=x[:], scalar=ng_sb[m][:, jl, 0:1],
+                    nc.vector.scalar_tensor_tensor(out=rmax[pc][:], in0=x[:], scalar=ng_sb[m][:, jl:jl + 1],
                                                    in1=rmax[pc][:], op0=ALU.add, op1=ALU.max)
 
-        def fold_partitions(g, tiles):
+        def fold_partitions(g, tiles, pc):
             bview = best[:].rearrange("p (b t) -> p t b", t=16)
-            for pc in range(NPC):
-                bank = psum.tile([P, 4, P], F32, name="tp")
-                for a in range(4):
-                    nc.tensor.transpose(bank[:, a, :], tiles[pc][:, a * P:(a + 1) * P], ident[:])
-                nc.vector.tensor_reduce(out=bview[:, 4 * pc:4 * pc + 4, GI * g:GI * (g + 1)],
-                                        in_=bank[:].rearrange("p a (i r) -> p a i r", i=GI),
-                                        axis=AX.X, op=ALU.max)
+            bank = psum.tile([P, 4, P], F32, name="tp")
+            for a in range(4):
+                nc.tensor.transpose(bank[:, a, :], tiles[pc][:, a * P:(a + 1) * P], ident[:])
+            nc.vector.tensor_reduce(out=bview[:, 4 * pc:4 * pc + 4, GI * g:GI * (g + 1)],
+                                    in_=bank[:].rearrange("p a (i r) -> p a i r", i=GI),
+                                    axis=AX.X, op=ALU.max)
 
         def p2_part(rt):
             nc.scalar.activation(out=junk[:], in_=proto_sb[:, rt, :], func=ACT.Square,
@@ -216,12 +214,13 @@ def tile_protopnet_pa_kernel(tc, h_relu, conv2_w, conv2_b, prototypes, out):
         fint(0, "g")
         hreg(1, "g", 0, 4)
         hreg(1, "g", 4, 8)
-        square(0)
+        for jl in range(4):
+            f2_tile(0, jl)
+        ngscale(0)
         words_to_mx(proto_sb, 4, pcodes[:, 512:1024], pscales[:, 512:1024], evac_v)
         quant_f(0)
         words_to_mx(proto_sb, 8, pcodes[:, 1024:1536], pscales[:, 1024:1536], evac_s)
         words_to_mx(proto_sb, 12, pcodes[:, 1536:2048], pscales[:, 1536:2048], evac_s)
-        ngmm(0)
 
         old = list(rmax)
         for k in range(NCHUNK):
@@ -231,8 +230,8 @@ def tile_protopnet_pa_kernel(tc, h_relu, conv2_w, conv2_b, prototypes, out):
                 if j == 0:
                     old = list(rmax)
                 st2(g, j)
-                if j == 0 and g > 0:
-                    fold_partitions(g - 1, old)
+                if g > 0 and s >= 2:
+                    fold_partitions(g - 1, old, 2 * (k % 2) + s - 2)
                 if k == 0 and s == 0:
                     for t in range(4):
                         st1(1, t)
@@ -244,10 +243,13 @@ def tile_protopnet_pa_kernel(tc, h_relu, conv2_w, conv2_b, prototypes, out):
                     st1(k + 2, s)
                 if k + 1 < NCHUNK:
                     if s == 0:
-                        square(k + 1)
                         fint(k + 1, "g")
+                    if s < 2:
+                        f2_tile(k + 1, 2 * s)
+                        f2_tile(k + 1, 2 * s + 1)
+                    if s == 1:
+                        ngscale(k + 1)
                     if s == 2:
-                        ngmm(k + 1)
                         quant_f(k + 1)
                 if k == 0:
                     if s == 1:
@@ -261,7 +263,8 @@ def tile_protopnet_pa_kernel(tc, h_relu, conv2_w, conv2_b, prototypes, out):
                 if s == 3:
                     p2_part(2 * k)
                     p2_part(2 * k + 1)
-        fold_partitions(NG - 1, rmax)
+        for pc in range(NPC):
+            fold_partitions(NG - 1, rmax, pc)
 
         res = const.tile([P, NIMG * 16], F32)
         nc.vector.scalar_tensor_tensor(

@@ -59,13 +59,10 @@ def tile_protopnet_pa_kernel(tc, h_relu, conv2_w, conv2_b, prototypes, out):
             )
 
         load_h(0)
-        load_proto(0)
-        load_proto(1)
-        load_h(1)
-        load_proto(2)
-        load_proto(3)
-        load_h(2)
-        load_h(3)
+        for pc in range(NPC):
+            load_proto(pc)
+        for g in range(1, NG):
+            load_h(g)
 
         ident = const.tile([P, P], F32)
         make_identity(nc, ident[:])
@@ -103,7 +100,7 @@ def tile_protopnet_pa_kernel(tc, h_relu, conv2_w, conv2_b, prototypes, out):
         def evac_v(o, i):
             nc.vector.tensor_copy(out=o, in_=i)
 
-        hg = [None] * NG
+        hg = [None] * NCHUNK
         hcodes = [None] * NCHUNK
         hscales = [None] * NCHUNK
         f32c = [None] * NCHUNK
@@ -114,24 +111,29 @@ def tile_protopnet_pa_kernel(tc, h_relu, conv2_w, conv2_b, prototypes, out):
         ng_sb = [None] * NCHUNK
         rmax = [None] * NPC
 
-        def hreg(g, eng, j0=0, j1=NJ):
-            if hg[g] is None:
-                hg[g] = work.tile([P, GI * HW * 4], BF16, name="hg", align_bytes=64)
-            dst = hg[g][:].rearrange("p (j i r c) -> p i j r c", j=NJ, i=GI, c=4)
+        def gp_tile():
+            return work.tile([P, 4 * CW], BF16, name="gp_out", bufs=1, align_bytes=64)
+
+        def hreg(m, eng):
+            g = m // 2
+            j0 = 4 * (m % 2)
+            if eng == "v":
+                hg[m] = work.tile([P, 4 * CW], BF16, name="hg_v", bufs=1, align_bytes=64)
+            else:
+                hg[m] = gp_tile()
+            dst = hg[m][:].rearrange("p (j i r c) -> p i j r c", j=4, i=GI, c=4)
             for i in range(GI):
-                src = h_sb[g][:, i, :].rearrange("p (c j r) -> p j r c", c=4, j=NJ)
+                src = h_sb[g][:, i, :].rearrange("p (c j r) -> p j r c", c=4, j=NJ)[:, j0:j0 + 4]
                 if eng == "v":
-                    nc.vector.tensor_copy(out=dst[:, i, j0:j1], in_=src[:, j0:j1])
+                    nc.vector.tensor_copy(out=dst[:, i], in_=src)
                 else:
-                    nc.gpsimd.tensor_scalar(out=dst[:, i, j0:j1], in0=src[:, j0:j1], scalar1=1.0,
+                    nc.gpsimd.tensor_scalar(out=dst[:, i], in0=src, scalar1=1.0,
                                             scalar2=0.0, op0=ALU.mult, op1=ALU.add)
 
         def quant_h(m):
             hcodes[m] = work.tile([P, CW], U32, name="hcodes", bufs=4, align_bytes=64)
             hscales[m] = work.tile([P, CW], U8, name="hscales", bufs=4, align_bytes=64)
-            half = m % 2
-            nc.vector.quantize_mx(out=hcodes[m][:].bitcast(FP8X4), scales=hscales[m][:],
-                                  in_=hg[m // 2][:, half * 4 * CW:(half + 1) * 4 * CW])
+            nc.vector.quantize_mx(out=hcodes[m][:].bitcast(FP8X4), scales=hscales[m][:], in_=hg[m][:])
 
         def st1(m, t):
             if t == 0:
@@ -158,7 +160,7 @@ def tile_protopnet_pa_kernel(tc, h_relu, conv2_w, conv2_b, prototypes, out):
             nc.scalar.mul(out=ng_sb[m][:], in_=f2c[m][:], mul=-0.5)
 
         def fint(m, eng):
-            fgc[m] = work.tile([P, 4 * CW], BF16, name="fgc", align_bytes=64)
+            fgc[m] = gp_tile()
             dst = fgc[m][:].rearrange("p (c t) -> p c t", t=4)
             src = f32c[m][:].rearrange("p t c -> p c t")
             if eng == "v":
@@ -204,23 +206,23 @@ def tile_protopnet_pa_kernel(tc, h_relu, conv2_w, conv2_b, prototypes, out):
                                  accum_out=p2_sb[:, rt:rt + 1])
 
         words_to_mx(w_sb, 0, wcodes[:], wscales[:], evac_s)
-        hreg(0, "v", 0, 4)
+        hreg(0, "v")
         quant_h(0)
-        hreg(0, "v", 4, 8)
-        quant_h(1)
+        hreg(1, "g")
         for t in range(4):
             st1(0, t)
         words_to_mx(proto_sb, 0, pcodes[:, 0:512], pscales[:, 0:512], evac_v)
+        quant_h(1)
         fint(0, "g")
-        hreg(1, "g", 0, 4)
-        hreg(1, "g", 4, 8)
         for jl in range(4):
             f2_tile(0, jl)
         ngscale(0)
         words_to_mx(proto_sb, 4, pcodes[:, 512:1024], pscales[:, 512:1024], evac_v)
         quant_f(0)
+        hreg(2, "g")
         words_to_mx(proto_sb, 8, pcodes[:, 1024:1536], pscales[:, 1024:1536], evac_s)
         words_to_mx(proto_sb, 12, pcodes[:, 1536:2048], pscales[:, 1536:2048], evac_s)
+        quant_h(2)
 
         old = list(rmax)
         for k in range(NCHUNK):
@@ -235,11 +237,7 @@ def tile_protopnet_pa_kernel(tc, h_relu, conv2_w, conv2_b, prototypes, out):
                 if k == 0 and s == 0:
                     for t in range(4):
                         st1(1, t)
-                if k == 0:
-                    if s >= 2:
-                        st1(2, 2 * s - 4)
-                        st1(2, 2 * s - 3)
-                elif k + 2 < NCHUNK:
+                if k + 2 < NCHUNK:
                     st1(k + 2, s)
                 if k + 1 < NCHUNK:
                     if s == 0:
@@ -249,17 +247,12 @@ def tile_protopnet_pa_kernel(tc, h_relu, conv2_w, conv2_b, prototypes, out):
                         f2_tile(k + 1, 2 * s + 1)
                     if s == 1:
                         ngscale(k + 1)
-                    if s == 2:
                         quant_f(k + 1)
-                if k == 0:
+                if k + 3 < NCHUNK:
                     if s == 1:
-                        quant_h(2)
+                        hreg(k + 3, "g")
                     if s == 3:
-                        quant_h(3)
-                elif s == 1 and k + 3 < NCHUNK:
-                    quant_h(k + 3)
-                if s == 1 and k % 2 == 0 and g + 2 < NG:
-                    hreg(g + 2, "g")
+                        quant_h(k + 3)
                 if s == 3:
                     p2_part(2 * k)
                     p2_part(2 * k + 1)

@@ -26,7 +26,7 @@ NCHUNK = NIMG * HW // CW
 NPC = NPROTO // 512
 
 FLOPS = 2 * CH * CH * NIMG * HW + 2 * NPROTO * CH * NIMG * HW
-MANUAL = False
+MANUAL = True
 
 
 def tile_protopnet_pa_kernel(tc, h_relu, conv2_w, conv2_b, prototypes, out):
@@ -82,7 +82,7 @@ def tile_protopnet_pa_kernel(tc, h_relu, conv2_w, conv2_b, prototypes, out):
             grouped = work.tile([P, 4 * 512], BF16, name="grouped", align_bytes=64)
             gw = grouped[:].bitcast(F32)
             for half in range(2):
-                bank = psum.tile([P, 2, 2, P], F32, name="tp")
+                bank = psum.tile([P, 2, 2, P], F32, name="x", bufs=5)
                 for a in range(2):
                     words = src[:, first_tile + 2 * half + a, :].bitcast(F32)
                     words = words.rearrange("r (q u) -> r u q", u=2)
@@ -109,7 +109,7 @@ def tile_protopnet_pa_kernel(tc, h_relu, conv2_w, conv2_b, prototypes, out):
         fcodes = [None] * NCHUNK
         fscales = [None] * NCHUNK
         ng_sb = [None] * NCHUNK
-        rmax = [None] * NPC
+        rmax = [[None] * NPC for g in range(NG)]
 
         def gp_tile():
             return work.tile([P, 4 * CW], BF16, name="gp_out", bufs=1, align_bytes=64)
@@ -138,7 +138,7 @@ def tile_protopnet_pa_kernel(tc, h_relu, conv2_w, conv2_b, prototypes, out):
         def st1(m, t):
             if t == 0:
                 f32c[m] = work.tile([P, 4, CW], F32, name="f32c", bufs=3)
-            z = psum.tile([P, CW], F32, name="z")
+            z = psum.tile([P, CW], F32, name="aux", bufs=3)
             nc.tensor.matmul_mx(out=z[:], lhsT=wcodes[:, t * P:(t + 1) * P].bitcast(FP8X4),
                                 lhsT_scale=wscales[:, t * P:(t + 1) * P],
                                 rhs=hcodes[m][:].bitcast(FP8X4), rhs_scale=hscales[m][:],
@@ -149,7 +149,7 @@ def tile_protopnet_pa_kernel(tc, h_relu, conv2_w, conv2_b, prototypes, out):
         def f2_tile(m, jl):
             if jl == 0:
                 f2c[m] = work.tile([P, 4], F32, name="f2c", bufs=4)
-            bank = psum.tile([P, 4, P], F32, name="tp")
+            bank = psum.tile([P, 4, P], F32, name="aux", bufs=3)
             for t in range(4):
                 nc.tensor.transpose(bank[:, t, :], f32c[m][:, t, jl * P:(jl + 1) * P], ident[:])
             nc.scalar.activation(out=junk32[:], in_=bank[:].rearrange("p t q -> p (t q)"), func=ACT.Square,
@@ -174,31 +174,32 @@ def tile_protopnet_pa_kernel(tc, h_relu, conv2_w, conv2_b, prototypes, out):
             fscales[m] = work.tile([P, CW], U8, name="fscales", bufs=4, align_bytes=64)
             nc.vector.quantize_mx(out=fcodes[m][:].bitcast(FP8X4), scales=fscales[m][:], in_=fgc[m][:])
 
-        def st2(g, j):
+        def tile2(g, j, pc):
             m = 2 * g + j // 4
             jl = j % 4
-            for pc in range(NPC):
-                x = psum.tile([P, 512], F32, name="x", bufs=4)
-                nc.tensor.matmul_mx(out=x[:], lhsT=fcodes[m][:, jl * P:(jl + 1) * P].bitcast(FP8X4),
-                                    lhsT_scale=fscales[m][:, jl * P:(jl + 1) * P],
-                                    rhs=pcodes[:, pc * 512:(pc + 1) * 512].bitcast(FP8X4),
-                                    rhs_scale=pscales[:, pc * 512:(pc + 1) * 512],
-                                    start=True, stop=True)
-                if j == 0:
-                    rmax[pc] = work.tile([P, 512], F32, name="rmax%d" % pc)
-                    nc.scalar.activation(out=rmax[pc][:], in_=x[:], func=ACT.Identity,
-                                         bias=ng_sb[m][:, jl:jl + 1], scale=1.0)
-                else:
-                    nc.vector.scalar_tensor_tensor(out=rmax[pc][:], in0=x[:], scalar=ng_sb[m][:, jl:jl + 1],
-                                                   in1=rmax[pc][:], op0=ALU.add, op1=ALU.max)
+            x = psum.tile([P, 512], F32, name="x", bufs=5)
+            nc.tensor.matmul_mx(out=x[:], lhsT=fcodes[m][:, jl * P:(jl + 1) * P].bitcast(FP8X4),
+                                lhsT_scale=fscales[m][:, jl * P:(jl + 1) * P],
+                                rhs=pcodes[:, pc * 512:(pc + 1) * 512].bitcast(FP8X4),
+                                rhs_scale=pscales[:, pc * 512:(pc + 1) * 512],
+                                start=True, stop=True)
+            if j == 0:
+                rmax[g][pc] = work.tile([P, 512], F32, name="rmax%d" % pc)
+                nc.scalar.activation(out=rmax[g][pc][:], in_=x[:], func=ACT.Identity,
+                                     bias=ng_sb[m][:, jl:jl + 1], scale=1.0)
+            else:
+                nc.vector.scalar_tensor_tensor(out=rmax[g][pc][:], in0=x[:], scalar=ng_sb[m][:, jl:jl + 1],
+                                               in1=rmax[g][pc][:], op0=ALU.add, op1=ALU.max)
 
-        def fold_partitions(g, tiles, pc):
+        def fold_partitions(g, pc):
             bview = best[:].rearrange("p (b t) -> p t b", t=16)
-            bank = psum.tile([P, 4, P], F32, name="tp")
+            bank = psum.tile([P, 4, P], F32, name="aux", bufs=3)
             for a in range(4):
-                nc.tensor.transpose(bank[:, a, :], tiles[pc][:, a * P:(a + 1) * P], ident[:])
+                nc.tensor.transpose(bank[:, a, :], rmax[g][pc][:, a * P:(a + 1) * P], ident[:])
+            flipped = work.tile([P, 4, P], F32, name="flipped")
+            nc.scalar.copy(out=flipped[:], in_=bank[:])
             nc.vector.tensor_reduce(out=bview[:, 4 * pc:4 * pc + 4, GI * g:GI * (g + 1)],
-                                    in_=bank[:].rearrange("p a (i r) -> p a i r", i=GI),
+                                    in_=flipped[:].rearrange("p a (i r) -> p a i r", i=GI),
                                     axis=AX.X, op=ALU.max)
 
         def p2_part(rt):
@@ -224,16 +225,23 @@ def tile_protopnet_pa_kernel(tc, h_relu, conv2_w, conv2_b, prototypes, out):
         words_to_mx(proto_sb, 12, pcodes[:, 1536:2048], pscales[:, 1536:2048], evac_s)
         quant_h(2)
 
-        old = list(rmax)
+        for pc in range(NPC):
+            tile2(0, 0, pc)
         for k in range(NCHUNK):
             g = k // 2
             for s in range(4):
                 j = 4 * (k % 2) + s
-                if j == 0:
-                    old = list(rmax)
-                st2(g, j)
+                if j == 7 and g + 1 < NG:
+                    for half in range(2):
+                        tile2(g, 7, 2 * half)
+                        tile2(g, 7, 2 * half + 1)
+                        tile2(g + 1, 0, 2 * half)
+                        tile2(g + 1, 0, 2 * half + 1)
+                elif j > 0:
+                    for pc in range(NPC):
+                        tile2(g, j, pc)
                 if g > 0 and s >= 2:
-                    fold_partitions(g - 1, old, 2 * (k % 2) + s - 2)
+                    fold_partitions(g - 1, 2 * (k % 2) + s - 2)
                 if k == 0 and s == 0:
                     for t in range(4):
                         st1(1, t)
@@ -253,11 +261,11 @@ def tile_protopnet_pa_kernel(tc, h_relu, conv2_w, conv2_b, prototypes, out):
                         hreg(k + 3, "g")
                     if s == 3:
                         quant_h(k + 3)
-                if s == 3:
-                    p2_part(2 * k)
-                    p2_part(2 * k + 1)
+                if k >= 6:
+                    p2_part(8 * (k - 6) + 2 * s)
+                    p2_part(8 * (k - 6) + 2 * s + 1)
         for pc in range(NPC):
-            fold_partitions(NG - 1, rmax, pc)
+            fold_partitions(NG - 1, pc)
 
         res = const.tile([P, NIMG * 16], F32)
         nc.vector.scalar_tensor_tensor(
@@ -266,7 +274,7 @@ def tile_protopnet_pa_kernel(tc, h_relu, conv2_w, conv2_b, prototypes, out):
             scalar=-2.0,
             in1=p2_sb[:].unsqueeze(1).to_broadcast([P, NIMG, 16]),
             op0=ALU.mult, op1=ALU.add)
-        tpf = psum.tile([P, 2, P], F32, name="tp")
+        tpf = psum.tile([P, 2, P], F32, name="aux", bufs=3)
         for hb in range(2):
             nc.tensor.transpose(tpf[:, hb, :], res[:, hb * P:(hb + 1) * P], ident[:])
         o_sb = const.tile([P, 2, P], F32)

@@ -78,9 +78,8 @@ def tile_protopnet_pa_kernel(tc, h_relu, conv2_w, conv2_b, prototypes, out):
         junk32 = const.tile([P, CH], BF16)
         best = const.tile([P, NIMG * 16], F32)
 
-        def words_to_mx(src, first_tile, codes, scales, evac):
-            grouped = work.tile([P, 4 * 512], BF16, name="grouped", align_bytes=64)
-            gw = grouped[:].bitcast(F32)
+        def words_transpose(src, first_tile):
+            banks = []
             for half in range(2):
                 bank = psum.tile([P, 2, 2, P], F32, name="x", bufs=5)
                 for a in range(2):
@@ -88,17 +87,26 @@ def tile_protopnet_pa_kernel(tc, h_relu, conv2_w, conv2_b, prototypes, out):
                     words = words.rearrange("r (q u) -> r u q", u=2)
                     for u in range(2):
                         nc.tensor.transpose(bank[:, a, u, :], words[:, u, :], ident[:])
-                evac(
-                    gw[:, half * 512:(half + 1) * 512].rearrange("q (a r u) -> q a r u", a=2, u=2),
-                    bank[:].rearrange("q a u r -> q a r u"),
-                )
+                banks.append(bank)
+            return banks
+
+        def words_copy(banks, eng):
+            grouped = work.tile([P, 4 * 512], BF16, name="grouped", align_bytes=64)
+            gw = grouped[:].bitcast(F32)
+            for half in range(2):
+                dst = gw[:, half * 512:(half + 1) * 512].rearrange("q (a r u) -> q a r u", a=2, u=2)
+                src = banks[half][:].rearrange("q a u r -> q a r u")
+                if eng == "v":
+                    nc.vector.tensor_copy(out=dst, in_=src)
+                else:
+                    nc.scalar.copy(out=dst, in_=src)
+            return grouped
+
+        def words_quant(grouped, codes, scales):
             nc.vector.quantize_mx(out=codes.bitcast(FP8X4), scales=scales, in_=grouped[:])
 
-        def evac_s(o, i):
-            nc.scalar.copy(out=o, in_=i)
-
-        def evac_v(o, i):
-            nc.vector.tensor_copy(out=o, in_=i)
+        def proto_cols(pc):
+            return pcodes[:, pc * 512:(pc + 1) * 512], pscales[:, pc * 512:(pc + 1) * 512]
 
         hg = [None] * NCHUNK
         hcodes = [None] * NCHUNK
@@ -177,7 +185,10 @@ def tile_protopnet_pa_kernel(tc, h_relu, conv2_w, conv2_b, prototypes, out):
         def tile2(g, j, pc):
             m = 2 * g + j // 4
             jl = j % 4
-            x = psum.tile([P, 512], F32, name="x", bufs=5)
+            if j == 0:
+                x = psum.tile([P, 512], F32, name="aux", bufs=3)
+            else:
+                x = psum.tile([P, 512], F32, name="x", bufs=5)
             nc.tensor.matmul_mx(out=x[:], lhsT=fcodes[m][:, jl * P:(jl + 1) * P].bitcast(FP8X4),
                                 lhsT_scale=fscales[m][:, jl * P:(jl + 1) * P],
                                 rhs=pcodes[:, pc * 512:(pc + 1) * 512].bitcast(FP8X4),
@@ -191,81 +202,116 @@ def tile_protopnet_pa_kernel(tc, h_relu, conv2_w, conv2_b, prototypes, out):
                 nc.vector.scalar_tensor_tensor(out=rmax[g][pc][:], in0=x[:], scalar=ng_sb[m][:, jl:jl + 1],
                                                in1=rmax[g][pc][:], op0=ALU.add, op1=ALU.max)
 
-        def fold_partitions(g, pc):
-            bview = best[:].rearrange("p (b t) -> p t b", t=16)
+        flipped = [[None] * NPC for g in range(NG)]
+
+        def fold_transpose(g, pc):
             bank = psum.tile([P, 4, P], F32, name="aux", bufs=3)
             for a in range(4):
                 nc.tensor.transpose(bank[:, a, :], rmax[g][pc][:, a * P:(a + 1) * P], ident[:])
-            flipped = work.tile([P, 4, P], F32, name="flipped")
-            nc.scalar.copy(out=flipped[:], in_=bank[:])
+            flipped[g][pc] = work.tile([P, 4, P], F32, name="flipped")
+            nc.scalar.copy(out=flipped[g][pc][:], in_=bank[:])
+
+        def fold_reduce(g, pc):
+            bview = best[:].rearrange("p (b t) -> p t b", t=16)
             nc.vector.tensor_reduce(out=bview[:, 4 * pc:4 * pc + 4, GI * g:GI * (g + 1)],
-                                    in_=flipped[:].rearrange("p a (i r) -> p a i r", i=GI),
+                                    in_=flipped[g][pc][:].rearrange("p a (i r) -> p a i r", i=GI),
                                     axis=AX.X, op=ALU.max)
 
         def p2_part(rt):
             nc.scalar.activation(out=junk[:], in_=proto_sb[:, rt, :], func=ACT.Square,
                                  accum_out=p2_sb[:, rt:rt + 1])
 
-        words_to_mx(w_sb, 0, wcodes[:], wscales[:], evac_s)
+        wb = words_transpose(w_sb, 0)
+        wg = words_copy(wb, "s")
+        words_quant(wg, wcodes[:], wscales[:])
         hreg(0, "v")
         quant_h(0)
         hreg(1, "g")
-        for t in range(4):
-            st1(0, t)
-        words_to_mx(proto_sb, 0, pcodes[:, 0:512], pscales[:, 0:512], evac_v)
+        pb0 = words_transpose(proto_sb, 0)
+        st1(0, 0)
+        st1(0, 1)
+        pg0 = words_copy(pb0, "v")
+        words_quant(pg0, *proto_cols(0))
+        pb1 = words_transpose(proto_sb, 4)
+        st1(0, 2)
+        st1(0, 3)
         quant_h(1)
+        pg1 = words_copy(pb1, "v")
+        words_quant(pg1, *proto_cols(1))
         fint(0, "g")
+        pb2 = words_transpose(proto_sb, 8)
+        st1(1, 0)
+        st1(1, 1)
         for jl in range(4):
             f2_tile(0, jl)
         ngscale(0)
-        words_to_mx(proto_sb, 4, pcodes[:, 512:1024], pscales[:, 512:1024], evac_v)
+        pg2 = words_copy(pb2, "v")
+        words_quant(pg2, *proto_cols(2))
+        pb3 = words_transpose(proto_sb, 12)
+        st1(1, 2)
+        st1(1, 3)
         quant_f(0)
-        hreg(2, "g")
-        words_to_mx(proto_sb, 8, pcodes[:, 1024:1536], pscales[:, 1024:1536], evac_s)
-        words_to_mx(proto_sb, 12, pcodes[:, 1536:2048], pscales[:, 1536:2048], evac_s)
-        quant_h(2)
-
+        fint(1, "g")
+        pg3 = words_copy(pb3, "v")
+        words_quant(pg3, *proto_cols(3))
         for pc in range(NPC):
             tile2(0, 0, pc)
-        for k in range(NCHUNK):
-            g = k // 2
-            for s in range(4):
-                j = 4 * (k % 2) + s
-                if j == 7 and g + 1 < NG:
-                    for half in range(2):
-                        tile2(g, 7, 2 * half)
-                        tile2(g, 7, 2 * half + 1)
-                        tile2(g + 1, 0, 2 * half)
-                        tile2(g + 1, 0, 2 * half + 1)
-                elif j > 0:
-                    for pc in range(NPC):
-                        tile2(g, j, pc)
-                if g > 0 and s >= 2:
-                    fold_partitions(g - 1, 2 * (k % 2) + s - 2)
-                if k == 0 and s == 0:
-                    for t in range(4):
-                        st1(1, t)
-                if k + 2 < NCHUNK:
-                    st1(k + 2, s)
-                if k + 1 < NCHUNK:
-                    if s == 0:
-                        fint(k + 1, "g")
-                    if s < 2:
-                        f2_tile(k + 1, 2 * s)
-                        f2_tile(k + 1, 2 * s + 1)
-                    if s == 1:
-                        ngscale(k + 1)
-                        quant_f(k + 1)
-                if k + 3 < NCHUNK:
-                    if s == 1:
-                        hreg(k + 3, "g")
-                    if s == 3:
-                        quant_h(k + 3)
-                if k >= 6:
-                    p2_part(8 * (k - 6) + 2 * s)
-                    p2_part(8 * (k - 6) + 2 * s + 1)
+
+        for u in range(4 * NCHUNK):
+            g = u // NJ
+            j = u % NJ
+            if j > 0:
+                for pc in range(NPC):
+                    tile2(g, j, pc)
+            if j == 6 and g + 1 < NG:
+                for pc in range(NPC):
+                    tile2(g + 1, 0, pc)
+            if u % 4 == 1:
+                c = (u + 3) // 4
+                if c < NCHUNK:
+                    quant_f(c)
+                    if c + 2 < NCHUNK:
+                        hreg(c + 2, "g")
+            if u % 4 == 3:
+                c = (u + 9) // 4
+                if c < NCHUNK:
+                    quant_h(c)
+                    fint(c - 1, "g")
+            if g > 0 and 2 <= j <= 5:
+                fold_reduce(g - 1, j - 2)
+            if g > 0 and 1 <= j <= 4:
+                fold_transpose(g - 1, j - 1)
+            if u % 4 == 1 and 2 <= (u + 7) // 4 < NCHUNK:
+                st1((u + 7) // 4, 0)
+                st1((u + 7) // 4, 1)
+            if u % 4 == 2 and 2 <= (u + 6) // 4 < NCHUNK:
+                st1((u + 6) // 4, 2)
+                st1((u + 6) // 4, 3)
+                if (u + 6) // 4 == NCHUNK - 1:
+                    fint(NCHUNK - 1, "g")
+            if u % 4 == 3 and 2 <= (u + 5) // 4 < NCHUNK:
+                f2_tile((u + 5) // 4, 0)
+                f2_tile((u + 5) // 4, 1)
+            if u % 4 == 0 and 2 <= (u + 4) // 4 < NCHUNK:
+                f2_tile((u + 4) // 4, 2)
+                f2_tile((u + 4) // 4, 3)
+                ngscale((u + 4) // 4)
+            if u == 0:
+                hreg(2, "v")
+                quant_h(2)
+            if u == 1:
+                f2_tile(1, 0)
+                f2_tile(1, 1)
+            if u == 2:
+                f2_tile(1, 2)
+                f2_tile(1, 3)
+                ngscale(1)
+            if u >= 24:
+                p2_part(2 * (u - 24))
+                p2_part(2 * (u - 24) + 1)
         for pc in range(NPC):
-            fold_partitions(NG - 1, pc)
+            fold_transpose(NG - 1, pc)
+            fold_reduce(NG - 1, pc)
 
         res = const.tile([P, NIMG * 16], F32)
         nc.vector.scalar_tensor_tensor(

@@ -81,7 +81,7 @@ def tile_protopnet_pa_kernel(tc, h_relu, conv2_w, conv2_b, prototypes, out):
         def words_transpose(src, first_tile):
             banks = []
             for half in range(2):
-                bank = psum.tile([P, 2, 2, P], F32, name="x", bufs=5)
+                bank = psum.tile([P, 2, 2, P], F32, name="x", bufs=4)
                 for a in range(2):
                     words = src[:, first_tile + 2 * half + a, :].bitcast(F32)
                     words = words.rearrange("r (q u) -> r u q", u=2)
@@ -146,7 +146,7 @@ def tile_protopnet_pa_kernel(tc, h_relu, conv2_w, conv2_b, prototypes, out):
         def st1(m, t):
             if t == 0:
                 f32c[m] = work.tile([P, 4, CW], F32, name="f32c", bufs=3)
-            z = psum.tile([P, CW], F32, name="aux", bufs=3)
+            z = psum.tile([P, CW], F32, name="aux", bufs=4)
             nc.tensor.matmul_mx(out=z[:], lhsT=wcodes[:, t * P:(t + 1) * P].bitcast(FP8X4),
                                 lhsT_scale=wscales[:, t * P:(t + 1) * P],
                                 rhs=hcodes[m][:].bitcast(FP8X4), rhs_scale=hscales[m][:],
@@ -157,7 +157,7 @@ def tile_protopnet_pa_kernel(tc, h_relu, conv2_w, conv2_b, prototypes, out):
         def f2_tile(m, jl):
             if jl == 0:
                 f2c[m] = work.tile([P, 4], F32, name="f2c", bufs=4)
-            bank = psum.tile([P, 4, P], F32, name="aux", bufs=3)
+            bank = psum.tile([P, 4, P], F32, name="aux", bufs=4)
             for t in range(4):
                 nc.tensor.transpose(bank[:, t, :], f32c[m][:, t, jl * P:(jl + 1) * P], ident[:])
             nc.scalar.activation(out=junk32[:], in_=bank[:].rearrange("p t q -> p (t q)"), func=ACT.Square,
@@ -186,9 +186,9 @@ def tile_protopnet_pa_kernel(tc, h_relu, conv2_w, conv2_b, prototypes, out):
             m = 2 * g + j // 4
             jl = j % 4
             if j == 0:
-                x = psum.tile([P, 512], F32, name="aux", bufs=3)
+                x = psum.tile([P, 512], F32, name="aux", bufs=4)
             else:
-                x = psum.tile([P, 512], F32, name="x", bufs=5)
+                x = psum.tile([P, 512], F32, name="x", bufs=4)
             nc.tensor.matmul_mx(out=x[:], lhsT=fcodes[m][:, jl * P:(jl + 1) * P].bitcast(FP8X4),
                                 lhsT_scale=fscales[m][:, jl * P:(jl + 1) * P],
                                 rhs=pcodes[:, pc * 512:(pc + 1) * 512].bitcast(FP8X4),
@@ -205,7 +205,7 @@ def tile_protopnet_pa_kernel(tc, h_relu, conv2_w, conv2_b, prototypes, out):
         flipped = [[None] * NPC for g in range(NG)]
 
         def fold_transpose(g, pc):
-            bank = psum.tile([P, 4, P], F32, name="aux", bufs=3)
+            bank = psum.tile([P, 4, P], F32, name="aux", bufs=4)
             for a in range(4):
                 nc.tensor.transpose(bank[:, a, :], rmax[g][pc][:, a * P:(a + 1) * P], ident[:])
             flipped[g][pc] = work.tile([P, 4, P], F32, name="flipped")
@@ -263,9 +263,6 @@ def tile_protopnet_pa_kernel(tc, h_relu, conv2_w, conv2_b, prototypes, out):
             if j > 0:
                 for pc in range(NPC):
                     tile2(g, j, pc)
-            if j == 6 and g + 1 < NG:
-                for pc in range(NPC):
-                    tile2(g + 1, 0, pc)
             if u % 4 == 1:
                 c = (u + 3) // 4
                 if c < NCHUNK:
@@ -309,6 +306,9 @@ def tile_protopnet_pa_kernel(tc, h_relu, conv2_w, conv2_b, prototypes, out):
             if u >= 24:
                 p2_part(2 * (u - 24))
                 p2_part(2 * (u - 24) + 1)
+            if j == 6 and g + 1 < NG:
+                for pc in range(NPC):
+                    tile2(g + 1, 0, pc)
         for pc in range(NPC):
             fold_transpose(NG - 1, pc)
             fold_reduce(NG - 1, pc)
@@ -320,7 +320,7 @@ def tile_protopnet_pa_kernel(tc, h_relu, conv2_w, conv2_b, prototypes, out):
             scalar=-2.0,
             in1=p2_sb[:].unsqueeze(1).to_broadcast([P, NIMG, 16]),
             op0=ALU.mult, op1=ALU.add)
-        tpf = psum.tile([P, 2, P], F32, name="aux", bufs=3)
+        tpf = psum.tile([P, 2, P], F32, name="aux", bufs=4)
         for hb in range(2):
             nc.tensor.transpose(tpf[:, hb, :], res[:, hb * P:(hb + 1) * P], ident[:])
         o_sb = const.tile([P, 2, P], F32)

@@ -208,8 +208,11 @@ def tile_protopnet_pa_kernel(tc, h_relu, conv2_w, conv2_b, prototypes, out):
             bank = psum.tile([P, 4, P], F32, name="aux", bufs=4)
             for a in range(4):
                 nc.tensor.transpose(bank[:, a, :], rmax[g][pc][:, a * P:(a + 1) * P], ident[:])
-            flipped[g][pc] = work.tile([P, 4, P], F32, name="flipped")
-            nc.scalar.copy(out=flipped[g][pc][:], in_=bank[:])
+            if g + 1 < NG:
+                flipped[g][pc] = work.tile([P, 4, P], F32, name="flipped")
+                nc.scalar.copy(out=flipped[g][pc][:], in_=bank[:])
+            else:
+                flipped[g][pc] = bank
 
         def fold_reduce(g, pc):
             bview = best[:].rearrange("p (b t) -> p t b", t=16)
@@ -228,13 +231,11 @@ def tile_protopnet_pa_kernel(tc, h_relu, conv2_w, conv2_b, prototypes, out):
         quant_h(0)
         hreg(1, "g")
         pb0 = words_transpose(proto_sb, 0)
-        st1(0, 0)
-        st1(0, 1)
+        for t in range(4):
+            st1(0, t)
         pg0 = words_copy(pb0, "v")
         words_quant(pg0, *proto_cols(0))
         pb1 = words_transpose(proto_sb, 4)
-        st1(0, 2)
-        st1(0, 3)
         quant_h(1)
         pg1 = words_copy(pb1, "v")
         words_quant(pg1, *proto_cols(1))
@@ -262,10 +263,17 @@ def tile_protopnet_pa_kernel(tc, h_relu, conv2_w, conv2_b, prototypes, out):
             j = u % NJ
             if j > 0:
                 for pc in range(NPC):
+                    if j == 7 and g + 1 < NG and pc == 2:
+                        tile2(g + 1, 0, 2)
+                        tile2(g + 1, 0, 3)
                     tile2(g, j, pc)
+                    if pc == 1 and j == 2 and g > 0:
+                        quant_f((u + 2) // 4)
+                        if (u + 2) // 4 + 2 < NCHUNK:
+                            hreg((u + 2) // 4 + 2, "g")
             if u % 4 == 1:
                 c = (u + 3) // 4
-                if c < NCHUNK:
+                if c < NCHUNK and (c % 2 == 0 or c == 1):
                     quant_f(c)
                     if c + 2 < NCHUNK:
                         hreg(c + 2, "g")
@@ -307,10 +315,11 @@ def tile_protopnet_pa_kernel(tc, h_relu, conv2_w, conv2_b, prototypes, out):
                 p2_part(2 * (u - 24))
                 p2_part(2 * (u - 24) + 1)
             if j == 6 and g + 1 < NG:
-                for pc in range(NPC):
-                    tile2(g + 1, 0, pc)
+                tile2(g + 1, 0, 0)
+                tile2(g + 1, 0, 1)
         for pc in range(NPC):
             fold_transpose(NG - 1, pc)
+        for pc in range(NPC):
             fold_reduce(NG - 1, pc)
 
         res = const.tile([P, NIMG * 16], F32)

@@ -45,12 +45,14 @@ def tile_protopnet_pa_kernel(tc, h_relu, conv2_w, conv2_b, prototypes, out):
         h_sb = [None] * NG
         proto_sb = const.tile([P, 16, CH], BF16)
 
-        def load_h(g):
+        def load_h(g, pieces):
             h_sb[g] = work.tile([P, GI, 4 * HW], BF16, name="h_sb", bufs=NG)
-            nc.sync.dma_start(
-                out=h_sb[g][:],
-                in_=h_relu[g * GI:(g + 1) * GI].rearrange("i (p j) y x -> p i (j y x)", j=4),
-            )
+            n = GI // pieces
+            for k in range(pieces):
+                nc.sync.dma_start(
+                    out=h_sb[g][:, k * n:(k + 1) * n],
+                    in_=h_relu[g * GI + k * n:g * GI + (k + 1) * n].rearrange("i (p j) y x -> p i (j y x)", j=4),
+                )
 
         def load_proto(pc):
             nc.sync.dma_start(
@@ -58,11 +60,11 @@ def tile_protopnet_pa_kernel(tc, h_relu, conv2_w, conv2_b, prototypes, out):
                 in_=prototypes[pc * 512:(pc + 1) * 512, :].rearrange("(a r) d -> r a d", r=P),
             )
 
-        load_h(0)
+        load_h(0, 2)
         for pc in range(NPC):
             load_proto(pc)
         for g in range(1, NG):
-            load_h(g)
+            load_h(g, 1)
 
         ident = const.tile([P, P], F32)
         make_identity(nc, ident[:])
@@ -117,20 +119,22 @@ def tile_protopnet_pa_kernel(tc, h_relu, conv2_w, conv2_b, prototypes, out):
         fcodes = [None] * NCHUNK
         fscales = [None] * NCHUNK
         ng_sb = [None] * NCHUNK
+        dng_sb = [None] * NCHUNK
         rmax = [[None] * NPC for g in range(NG)]
 
         def gp_tile():
-            return work.tile([P, 4 * CW], BF16, name="gp_out", bufs=1, align_bytes=64)
+            return work.tile([P, 5 * CW], BF16, name="gp_out", bufs=2, align_bytes=64)
 
-        def hreg(m, eng):
+        def hreg(m, eng, images=range(GI)):
             g = m // 2
             j0 = 4 * (m % 2)
-            if eng == "v":
-                hg[m] = work.tile([P, 4 * CW], BF16, name="hg_v", bufs=1, align_bytes=64)
-            else:
-                hg[m] = gp_tile()
-            dst = hg[m][:].rearrange("p (j i r c) -> p i j r c", j=4, i=GI, c=4)
-            for i in range(GI):
+            if hg[m] is None:
+                if eng == "v":
+                    hg[m] = work.tile([P, 4 * CW], BF16, name="hg_v", bufs=1, align_bytes=64)
+                else:
+                    hg[m] = gp_tile()
+            dst = hg[m][:, :4 * CW].rearrange("p (j i r c) -> p i j r c", j=4, i=GI, c=4)
+            for i in images:
                 src = h_sb[g][:, i, :].rearrange("p (c j r) -> p j r c", c=4, j=NJ)[:, j0:j0 + 4]
                 if eng == "v":
                     nc.vector.tensor_copy(out=dst[:, i], in_=src)
@@ -141,7 +145,7 @@ def tile_protopnet_pa_kernel(tc, h_relu, conv2_w, conv2_b, prototypes, out):
         def quant_h(m):
             hcodes[m] = work.tile([P, CW], U32, name="hcodes", bufs=4, align_bytes=64)
             hscales[m] = work.tile([P, CW], U8, name="hscales", bufs=4, align_bytes=64)
-            nc.vector.quantize_mx(out=hcodes[m][:].bitcast(FP8X4), scales=hscales[m][:], in_=hg[m][:])
+            nc.vector.quantize_mx(out=hcodes[m][:].bitcast(FP8X4), scales=hscales[m][:], in_=hg[m][:, :4 * CW])
 
         def st1(m, t):
             if t == 0:
@@ -162,62 +166,88 @@ def tile_protopnet_pa_kernel(tc, h_relu, conv2_w, conv2_b, prototypes, out):
                 nc.tensor.transpose(bank[:, t, :], f32c[m][:, t, jl * P:(jl + 1) * P], ident[:])
             nc.scalar.activation(out=junk32[:], in_=bank[:].rearrange("p t q -> p (t q)"), func=ACT.Square,
                                  accum_out=f2c[m][:, jl:jl + 1])
+            if jl == 3:
+                ng_sb[m] = work.tile([P, 4], F32, name="ng_sb", bufs=4)
+                nc.scalar.mul(out=ng_sb[m][:], in_=f2c[m][:], mul=-0.5)
+                if paired(m):
+                    dng_sb[m] = work.tile([P, 1], F32, name="dng_sb", bufs=2)
+                    nc.scalar.activation(out=dng_sb[m][:], in_=f2c[m][:, 1:2], func=ACT.Identity,
+                                         bias=ng_sb[m][:, 0:1], scale=0.5)
 
-        def ngscale(m):
-            ng_sb[m] = work.tile([P, 4], F32, name="ng_sb", bufs=4)
-            nc.scalar.mul(out=ng_sb[m][:], in_=f2c[m][:], mul=-0.5)
+        def paired(m):
+            return m % 2 == 0 and m > 0
 
         def fint(m, eng):
-            fgc[m] = gp_tile()
-            dst = fgc[m][:].rearrange("p (c t) -> p c t", t=4)
+            if eng == "v":
+                fgc[m] = work.tile([P, 4 * CW], BF16, name="fg_v", bufs=1, align_bytes=64)
+            else:
+                fgc[m] = gp_tile()
+            dst = fgc[m][:, :4 * CW].rearrange("p (c t) -> p c t", t=4)
             src = f32c[m][:].rearrange("p t c -> p c t")
             if eng == "v":
                 nc.vector.tensor_copy(out=dst, in_=src)
             else:
                 nc.gpsimd.tensor_scalar(out=dst, in0=src, scalar1=1.0, scalar2=0.0,
                                         op0=ALU.mult, op1=ALU.add)
+                if paired(m):
+                    nc.gpsimd.tensor_scalar(
+                        out=fgc[m][:, 4 * CW:].rearrange("p (c t) -> p c t", t=4),
+                        in0=f32c[m][:, :, P:2 * P].rearrange("p t c -> p c t"),
+                        scalar1=-1.0, scalar2=0.0, op0=ALU.mult, op1=ALU.add)
 
         def quant_f(m):
-            fcodes[m] = work.tile([P, CW], U32, name="fcodes", bufs=4, align_bytes=64)
-            fscales[m] = work.tile([P, CW], U8, name="fscales", bufs=4, align_bytes=64)
-            nc.vector.quantize_mx(out=fcodes[m][:].bitcast(FP8X4), scales=fscales[m][:], in_=fgc[m][:])
+            width = CW + P
+            fcodes[m] = work.tile([P, width], U32, name="fcodes", bufs=4, align_bytes=64)
+            fscales[m] = work.tile([P, width], U8, name="fscales", bufs=4, align_bytes=64)
+            nc.vector.quantize_mx(out=fcodes[m][:, :CW].bitcast(FP8X4), scales=fscales[m][:, :CW],
+                                  in_=fgc[m][:, :4 * CW])
+            if paired(m):
+                nc.vector.quantize_mx(out=fcodes[m][:, CW:].bitcast(FP8X4), scales=fscales[m][:, CW:],
+                                      in_=fgc[m][:, 4 * CW:])
 
-        def tile2(g, j, pc):
-            m = 2 * g + j // 4
-            jl = j % 4
-            if j == 0:
-                x = psum.tile([P, 512], F32, name="aux", bufs=4)
-            else:
-                x = psum.tile([P, 512], F32, name="x", bufs=4)
+        def fp_pass(x, m, jl, pc, start=True, stop=True):
             nc.tensor.matmul_mx(out=x[:], lhsT=fcodes[m][:, jl * P:(jl + 1) * P].bitcast(FP8X4),
                                 lhsT_scale=fscales[m][:, jl * P:(jl + 1) * P],
                                 rhs=pcodes[:, pc * 512:(pc + 1) * 512].bitcast(FP8X4),
                                 rhs_scale=pscales[:, pc * 512:(pc + 1) * 512],
-                                start=True, stop=True)
-            if j == 0:
-                rmax[g][pc] = work.tile([P, 512], F32, name="rmax%d" % pc)
-                nc.scalar.activation(out=rmax[g][pc][:], in_=x[:], func=ACT.Identity,
-                                     bias=ng_sb[m][:, jl:jl + 1], scale=1.0)
-            else:
-                nc.vector.scalar_tensor_tensor(out=rmax[g][pc][:], in0=x[:], scalar=ng_sb[m][:, jl:jl + 1],
-                                               in1=rmax[g][pc][:], op0=ALU.add, op1=ALU.max)
+                                start=start, stop=stop)
 
-        flipped = [[None] * NPC for g in range(NG)]
+        def first(g, pc):
+            x = psum.tile([P, 512], F32, name="aux", bufs=4)
+            fp_pass(x, 2 * g, 0, pc)
+            rmax[g][pc] = work.tile([P, 512], F32, name="rmax%d" % pc)
+            nc.scalar.activation(out=rmax[g][pc][:], in_=x[:], func=ACT.Identity,
+                                 bias=ng_sb[2 * g][:, 0:1], scale=1.0)
 
-        def fold_transpose(g, pc):
-            bank = psum.tile([P, 4, P], F32, name="aux", bufs=4)
+        def pair(g, pc):
+            m = 2 * g
+            xd = psum.tile([P, 512], F32, name="aux", bufs=4)
+            fp_pass(xd, m, 0, pc, start=True, stop=False)
+            fp_pass(xd, m, 4, pc, start=False, stop=True)
+            dd = work.tile([P, 512], F32, name="dd", bufs=4)
+            nc.scalar.activation(out=dd[:], in_=xd[:], func=ACT.Relu, bias=dng_sb[m][:], scale=1.0)
+            xb = psum.tile([P, 512], F32, name="aux", bufs=4)
+            fp_pass(xb, m, 1, pc)
+            rmax[g][pc] = work.tile([P, 512], F32, name="rmax%d" % pc)
+            nc.scalar.activation(out=rmax[g][pc][:], in_=xb[:], func=ACT.Identity,
+                                 bias=ng_sb[m][:, 1:2], scale=1.0)
+            nc.gpsimd.tensor_tensor(out=rmax[g][pc][:], in0=rmax[g][pc][:], in1=dd[:], op=ALU.add)
+
+        def tile2(g, j, pc):
+            m = 2 * g + j // 4
+            jl = j % 4
+            x = psum.tile([P, 512], F32, name="x", bufs=4)
+            fp_pass(x, m, jl, pc)
+            nc.vector.scalar_tensor_tensor(out=rmax[g][pc][:], in0=x[:], scalar=ng_sb[m][:, jl:jl + 1],
+                                           in1=rmax[g][pc][:], op0=ALU.add, op1=ALU.max)
+
+        def fold(g, pc):
+            bank = psum.tile([P, 4, P], F32, name="x", bufs=4)
             for a in range(4):
                 nc.tensor.transpose(bank[:, a, :], rmax[g][pc][:, a * P:(a + 1) * P], ident[:])
-            if g + 1 < NG:
-                flipped[g][pc] = work.tile([P, 4, P], F32, name="flipped")
-                nc.scalar.copy(out=flipped[g][pc][:], in_=bank[:])
-            else:
-                flipped[g][pc] = bank
-
-        def fold_reduce(g, pc):
             bview = best[:].rearrange("p (b t) -> p t b", t=16)
             nc.vector.tensor_reduce(out=bview[:, 4 * pc:4 * pc + 4, GI * g:GI * (g + 1)],
-                                    in_=flipped[g][pc][:].rearrange("p a (i r) -> p a i r", i=GI),
+                                    in_=bank[:].rearrange("p a (i r) -> p a i r", i=GI),
                                     axis=AX.X, op=ALU.max)
 
         def p2_part(rt):
@@ -226,114 +256,121 @@ def tile_protopnet_pa_kernel(tc, h_relu, conv2_w, conv2_b, prototypes, out):
 
         wb = words_transpose(w_sb, 0)
         wg = words_copy(wb, "s")
+        hreg(0, "v", [0, 1])
+        hreg(0, "v", [2, 3])
         words_quant(wg, wcodes[:], wscales[:])
-        hreg(0, "v")
         quant_h(0)
         hreg(1, "g")
-        pb0 = words_transpose(proto_sb, 0)
+        pb = words_transpose(proto_sb, 0)
+        pg0 = words_copy(pb, "s")
         for t in range(4):
             st1(0, t)
-        pg0 = words_copy(pb0, "v")
-        words_quant(pg0, *proto_cols(0))
-        pb1 = words_transpose(proto_sb, 4)
         quant_h(1)
-        pg1 = words_copy(pb1, "v")
+        hreg(2, "g")
+        pb = words_transpose(proto_sb, 4)
+        pg1 = words_copy(pb, "v")
+        fint(0, "v")
+        words_quant(pg0, *proto_cols(0))
+        quant_f(0)
         words_quant(pg1, *proto_cols(1))
-        fint(0, "g")
-        pb2 = words_transpose(proto_sb, 8)
-        st1(1, 0)
-        st1(1, 1)
         for jl in range(4):
             f2_tile(0, jl)
-        ngscale(0)
-        pg2 = words_copy(pb2, "v")
+        pb = words_transpose(proto_sb, 8)
+        pg2 = words_copy(pb, "v")
+        first(0, 0)
+        first(0, 1)
+        tile2(0, 1, 0)
         words_quant(pg2, *proto_cols(2))
-        pb3 = words_transpose(proto_sb, 12)
+        tile2(0, 1, 1)
+        st1(1, 0)
+        st1(1, 1)
+        pb = words_transpose(proto_sb, 12)
+        pg3 = words_copy(pb, "v")
+        first(0, 2)
+        tile2(0, 1, 2)
         st1(1, 2)
         st1(1, 3)
-        quant_f(0)
-        fint(1, "g")
-        pg3 = words_copy(pb3, "v")
         words_quant(pg3, *proto_cols(3))
-        for pc in range(NPC):
-            tile2(0, 0, pc)
+        tile2(0, 2, 0)
+        tile2(0, 2, 1)
+        first(0, 3)
+        tile2(0, 1, 3)
+        f2_tile(1, 0)
+        f2_tile(1, 1)
+        quant_h(2)
+        fint(1, "g")
+        hreg(3, "g")
+        tile2(0, 2, 2)
+        tile2(0, 2, 3)
+        f2_tile(1, 2)
+        f2_tile(1, 3)
 
-        for u in range(4 * NCHUNK):
-            g = u // NJ
-            j = u % NJ
-            if j > 0:
-                for pc in range(NPC):
-                    if j == 7 and g + 1 < NG and pc == 2:
-                        tile2(g + 1, 0, 2)
-                        tile2(g + 1, 0, 3)
-                    tile2(g, j, pc)
-                    if pc == 1 and j == 2 and g > 0:
-                        quant_f((u + 2) // 4)
-                        if (u + 2) // 4 + 2 < NCHUNK:
-                            hreg((u + 2) // 4 + 2, "g")
-            if u % 4 == 1:
-                c = (u + 3) // 4
-                if c < NCHUNK and (c % 2 == 0 or c == 1):
-                    quant_f(c)
-                    if c + 2 < NCHUNK:
-                        hreg(c + 2, "g")
-            if u % 4 == 3:
-                c = (u + 9) // 4
-                if c < NCHUNK:
-                    quant_h(c)
-                    fint(c - 1, "g")
-            if g > 0 and 2 <= j <= 5:
-                fold_reduce(g - 1, j - 2)
-            if g > 0 and 1 <= j <= 4:
-                fold_transpose(g - 1, j - 1)
-            if u % 4 == 1 and 2 <= (u + 7) // 4 < NCHUNK:
-                st1((u + 7) // 4, 0)
-                st1((u + 7) // 4, 1)
-            if u % 4 == 2 and 2 <= (u + 6) // 4 < NCHUNK:
-                st1((u + 6) // 4, 2)
-                st1((u + 6) // 4, 3)
-                if (u + 6) // 4 == NCHUNK - 1:
-                    fint(NCHUNK - 1, "g")
-            if u % 4 == 3 and 2 <= (u + 5) // 4 < NCHUNK:
-                f2_tile((u + 5) // 4, 0)
-                f2_tile((u + 5) // 4, 1)
-            if u % 4 == 0 and 2 <= (u + 4) // 4 < NCHUNK:
-                f2_tile((u + 4) // 4, 2)
-                f2_tile((u + 4) // 4, 3)
-                ngscale((u + 4) // 4)
-            if u == 0:
-                hreg(2, "v")
-                quant_h(2)
-            if u == 1:
-                f2_tile(1, 0)
-                f2_tile(1, 1)
-            if u == 2:
-                f2_tile(1, 2)
-                f2_tile(1, 3)
-                ngscale(1)
-            if u >= 24:
-                p2_part(2 * (u - 24))
-                p2_part(2 * (u - 24) + 1)
-            if j == 6 and g + 1 < NG:
-                tile2(g + 1, 0, 0)
-                tile2(g + 1, 0, 1)
-        for pc in range(NPC):
-            fold_transpose(NG - 1, pc)
-        for pc in range(NPC):
-            fold_reduce(NG - 1, pc)
+        for g in range(NG):
+            plan = [[] for k in range(24)]
+            odd = 2 * g + 1
+            even_next = odd + 1
+            odd_next = odd + 2
+            if g > 0:
+                plan[1].append(lambda: fold(g - 1, 0))
+                plan[3].append(lambda: fold(g - 1, 1))
+                for k in range(4):
+                    plan[1 + 2 * (k // 2)].append(lambda k=k: f2_tile(odd, k))
+                fold_at = 9 if g + 1 < NG else 5
+                plan[fold_at].append(lambda: fold(g - 1, 2))
+                plan[fold_at + 2].append(lambda: fold(g - 1, 3))
+            else:
+                plan[5].append(lambda: quant_f(1))
+            if g + 1 < NG:
+                if g > 0:
+                    plan[1].append(lambda: hreg(odd_next, "g"))
+                for k in range(4):
+                    plan[5 + 2 * (k // 2)].append(lambda k=k: st1(even_next, k))
+                plan[7].append(lambda: fint(even_next, "g"))
+                for k in range(4):
+                    plan[9 + 2 * (k // 2)].append(lambda k=k: f2_tile(even_next, k))
+                plan[10].append(lambda: quant_h(odd_next))
+                for k in range(4):
+                    plan[13 + 2 * (k // 2)].append(lambda k=k: st1(odd_next, k))
+                plan[14].append(lambda: quant_f(even_next))
+                if odd_next + 1 < NCHUNK:
+                    plan[14].append(lambda: hreg(odd_next + 1, "g"))
+                plan[15].append(lambda: fint(odd_next, "g"))
+                for k in range(4):
+                    plan[17 + 2 * k].append(lambda k=k: pair(g + 1, k))
+                if odd_next + 1 < NCHUNK:
+                    plan[18].append(lambda: quant_h(odd_next + 1))
+                plan[22].append(lambda: quant_f(odd_next))
+            for k in range(0 if g > 0 else 4, 24 if g + 1 < NG else 8):
+                tile2(g, 2 + k // 4, k % 4)
+                for f in plan[k]:
+                    f()
 
-        res = const.tile([P, NIMG * 16], F32)
-        nc.vector.scalar_tensor_tensor(
-            out=res[:].rearrange("p (b t) -> p b t", t=16),
-            in0=best[:].rearrange("p (b t) -> p b t", t=16),
-            scalar=-2.0,
-            in1=p2_sb[:].unsqueeze(1).to_broadcast([P, NIMG, 16]),
-            op0=ALU.mult, op1=ALU.add)
-        tpf = psum.tile([P, 2, P], F32, name="aux", bufs=4)
-        for hb in range(2):
-            nc.tensor.transpose(tpf[:, hb, :], res[:, hb * P:(hb + 1) * P], ident[:])
-        o_sb = const.tile([P, 2, P], F32)
-        nc.vector.tensor_copy(out=o_sb[:], in_=tpf[:])
-        nc.sync.dma_start(
-            out=out.rearrange("b (t p) -> (b t) p", p=P).rearrange("(h c) p -> c h p", h=2),
-            in_=o_sb[:])
+        last = NG - 1
+        for j in range(4, NJ):
+            tile2(last, j, 0)
+            tile2(last, j, 1)
+            for k in range(4):
+                p2_part(4 * (j - 4) + k)
+        for j in range(4, NJ):
+            tile2(last, j, 2)
+            tile2(last, j, 3)
+            if j < 6:
+                fold(last, j - 4)
+        fold(last, 2)
+        fold(last, 3)
+
+        for half in range(2):
+            res = const.tile([P, P], F32, name="res%d" % half)
+            nc.vector.scalar_tensor_tensor(
+                out=res[:].rearrange("p (b t) -> p b t", t=16),
+                in0=best[:, half * P:(half + 1) * P].rearrange("p (b t) -> p b t", t=16),
+                scalar=-2.0,
+                in1=p2_sb[:].unsqueeze(1).to_broadcast([P, 8, 16]),
+                op0=ALU.mult, op1=ALU.add)
+            tpf = psum.tile([P, P], F32, name="aux", bufs=4)
+            nc.tensor.transpose(tpf[:], res[:], ident[:])
+            o_sb = const.tile([P, P], F32, name="o_sb%d" % half)
+            nc.scalar.copy(out=o_sb[:], in_=tpf[:])
+            nc.sync.dma_start(
+                out=out.rearrange("b (t p) -> (b t) p", p=P)[half * P:(half + 1) * P, :],
+                in_=o_sb[:])

@@ -175,7 +175,7 @@ def tile_protopnet_pa_kernel(tc, h_relu, conv2_w, conv2_b, prototypes, out):
                                          bias=ng_sb[m][:, 0:1], scale=0.5)
 
         def paired(m):
-            return m % 2 == 0 and m > 0
+            return False
 
         def fint(m, eng):
             if eng == "v":
@@ -336,10 +336,13 @@ def tile_protopnet_pa_kernel(tc, h_relu, conv2_w, conv2_b, prototypes, out):
                     plan[14].append(lambda: hreg(odd_next + 1, "g"))
                 plan[15].append(lambda: fint(odd_next, "g"))
                 for k in range(4):
-                    plan[17 + 2 * k].append(lambda k=k: pair(g + 1, k))
+                    plan[17 + 2 * k].append(lambda k=k: first(g + 1, k))
                 if odd_next + 1 < NCHUNK:
                     plan[18].append(lambda: quant_h(odd_next + 1))
                 plan[22].append(lambda: quant_f(odd_next))
+            if g > 0:
+                for pc in range(NPC):
+                    tile2(g, 1, pc)
             for k in range(0 if g > 0 else 4, 24 if g + 1 < NG else 8):
                 tile2(g, 2 + k // 4, k % 4)
                 for f in plan[k]:

@@ -92,9 +92,10 @@ def tile_protopnet_pa_kernel(tc, h_relu, conv2_w, conv2_b, prototypes, out):
                 banks.append(bank)
             return banks
 
-        def words_copy(banks, eng):
-            grouped = work.tile([P, 4 * 512], BF16, name="grouped", align_bytes=64)
-            gw = grouped[:].bitcast(F32)
+        def words_copy(banks, eng, grouped=None):
+            if grouped is None:
+                grouped = work.tile([P, 4 * 512], BF16, name="grouped", align_bytes=64)
+            gw = grouped[:, :4 * 512].bitcast(F32)
             for half in range(2):
                 dst = gw[:, half * 512:(half + 1) * 512].rearrange("q (a r u) -> q a r u", a=2, u=2)
                 src = banks[half][:].rearrange("q a u r -> q a r u")
@@ -105,7 +106,7 @@ def tile_protopnet_pa_kernel(tc, h_relu, conv2_w, conv2_b, prototypes, out):
             return grouped
 
         def words_quant(grouped, codes, scales):
-            nc.vector.quantize_mx(out=codes.bitcast(FP8X4), scales=scales, in_=grouped[:])
+            nc.vector.quantize_mx(out=codes.bitcast(FP8X4), scales=scales, in_=grouped[:, :4 * 512])
 
         def proto_cols(pc):
             return pcodes[:, pc * 512:(pc + 1) * 512], pscales[:, pc * 512:(pc + 1) * 512]
@@ -123,21 +124,23 @@ def tile_protopnet_pa_kernel(tc, h_relu, conv2_w, conv2_b, prototypes, out):
         rmax = [[None] * NPC for g in range(NG)]
 
         def gp_tile():
-            return work.tile([P, 5 * CW], BF16, name="gp_out", bufs=2, align_bytes=64)
+            return work.tile([P, 5 * CW], BF16, name="gp_out", bufs=1, align_bytes=64)
 
         def hreg(m, eng, images=range(GI)):
             g = m // 2
             j0 = 4 * (m % 2)
             if hg[m] is None:
-                if eng == "v":
-                    hg[m] = work.tile([P, 4 * CW], BF16, name="hg_v", bufs=1, align_bytes=64)
-                else:
+                if eng == "g":
                     hg[m] = gp_tile()
+                else:
+                    hg[m] = work.tile([P, 4 * CW], BF16, name="hg_" + eng, bufs=1, align_bytes=64)
             dst = hg[m][:, :4 * CW].rearrange("p (j i r c) -> p i j r c", j=4, i=GI, c=4)
             for i in images:
                 src = h_sb[g][:, i, :].rearrange("p (c j r) -> p j r c", c=4, j=NJ)[:, j0:j0 + 4]
                 if eng == "v":
                     nc.vector.tensor_copy(out=dst[:, i], in_=src)
+                elif eng == "s":
+                    nc.scalar.copy(out=dst[:, i], in_=src)
                 else:
                     nc.gpsimd.tensor_scalar(out=dst[:, i], in0=src, scalar1=1.0,
                                             scalar2=0.0, op0=ALU.mult, op1=ALU.add)
@@ -215,7 +218,7 @@ def tile_protopnet_pa_kernel(tc, h_relu, conv2_w, conv2_b, prototypes, out):
         def first(g, pc):
             x = psum.tile([P, 512], F32, name="aux", bufs=4)
             fp_pass(x, 2 * g, 0, pc)
-            rmax[g][pc] = work.tile([P, 512], F32, name="rmax%d" % pc)
+            rmax[g][pc] = work.tile([P, 512], F32, name="rmax%d" % pc, bufs=3)
             nc.scalar.activation(out=rmax[g][pc][:], in_=x[:], func=ACT.Identity,
                                  bias=ng_sb[2 * g][:, 0:1], scale=1.0)
 
@@ -228,7 +231,7 @@ def tile_protopnet_pa_kernel(tc, h_relu, conv2_w, conv2_b, prototypes, out):
             nc.scalar.activation(out=dd[:], in_=xd[:], func=ACT.Relu, bias=dng_sb[m][:], scale=1.0)
             xb = psum.tile([P, 512], F32, name="aux", bufs=4)
             fp_pass(xb, m, 1, pc)
-            rmax[g][pc] = work.tile([P, 512], F32, name="rmax%d" % pc)
+            rmax[g][pc] = work.tile([P, 512], F32, name="rmax%d" % pc, bufs=3)
             nc.scalar.activation(out=rmax[g][pc][:], in_=xb[:], func=ACT.Identity,
                                  bias=ng_sb[m][:, 1:2], scale=1.0)
             nc.gpsimd.tensor_tensor(out=rmax[g][pc][:], in0=rmax[g][pc][:], in1=dd[:], op=ALU.add)
@@ -260,91 +263,70 @@ def tile_protopnet_pa_kernel(tc, h_relu, conv2_w, conv2_b, prototypes, out):
         hreg(0, "v", [2, 3])
         words_quant(wg, wcodes[:], wscales[:])
         quant_h(0)
-        hreg(1, "g")
         pb = words_transpose(proto_sb, 0)
         pg0 = words_copy(pb, "s")
+        hreg(1, "v")
+        pb = words_transpose(proto_sb, 4)
+        pg1 = words_copy(pb, "v")
         for t in range(4):
             st1(0, t)
         quant_h(1)
-        hreg(2, "g")
-        pb = words_transpose(proto_sb, 4)
-        pg1 = words_copy(pb, "v")
-        fint(0, "v")
         words_quant(pg0, *proto_cols(0))
-        quant_f(0)
         words_quant(pg1, *proto_cols(1))
-        for jl in range(4):
-            f2_tile(0, jl)
+        fint(0, "v")
         pb = words_transpose(proto_sb, 8)
         pg2 = words_copy(pb, "v")
-        first(0, 0)
-        first(0, 1)
-        tile2(0, 1, 0)
+        quant_f(0)
         words_quant(pg2, *proto_cols(2))
-        tile2(0, 1, 1)
-        st1(1, 0)
-        st1(1, 1)
+        for jl in range(4):
+            f2_tile(0, jl)
         pb = words_transpose(proto_sb, 12)
-        pg3 = words_copy(pb, "v")
-        first(0, 2)
-        tile2(0, 1, 2)
-        st1(1, 2)
-        st1(1, 3)
-        words_quant(pg3, *proto_cols(3))
-        tile2(0, 2, 0)
-        tile2(0, 2, 1)
-        first(0, 3)
-        tile2(0, 1, 3)
-        f2_tile(1, 0)
-        f2_tile(1, 1)
-        quant_h(2)
-        fint(1, "g")
-        hreg(3, "g")
-        tile2(0, 2, 2)
-        tile2(0, 2, 3)
-        f2_tile(1, 2)
-        f2_tile(1, 3)
+        pg3 = words_copy(pb, "v", gp_tile())
+        for pc in range(NPC):
+            first(0, pc)
+            if pc == 0:
+                words_quant(pg3, *proto_cols(3))
+                hreg(2, "g")
 
         for g in range(NG):
-            plan = [[] for k in range(24)]
+            plan = [[] for k in range(28)]
             odd = 2 * g + 1
-            even_next = odd + 1
-            odd_next = odd + 2
-            if g > 0:
-                plan[1].append(lambda: fold(g - 1, 0))
-                plan[3].append(lambda: fold(g - 1, 1))
+            e = odd + 1
+            o = odd + 2
+            more = g + 1 < NG
+            if g == 0:
                 for k in range(4):
-                    plan[1 + 2 * (k // 2)].append(lambda k=k: f2_tile(odd, k))
-                fold_at = 9 if g + 1 < NG else 5
-                plan[fold_at].append(lambda: fold(g - 1, 2))
-                plan[fold_at + 2].append(lambda: fold(g - 1, 3))
+                    plan[0 + k].append(lambda k=k: st1(1, k))
+                plan[5].append(lambda: quant_h(2))
+                plan[5].append(lambda: fint(1, "g"))
+                qf_odd, qh_o, qf_e, qh_ne, late = 10, 15, 20, 25, 4
             else:
-                plan[5].append(lambda: quant_f(1))
-            if g + 1 < NG:
-                if g > 0:
-                    plan[1].append(lambda: hreg(odd_next, "g"))
+                qf_odd, qh_o, qf_e, qh_ne, late = 3, 10, 16, 22, 0
                 for k in range(4):
-                    plan[5 + 2 * (k // 2)].append(lambda k=k: st1(even_next, k))
-                plan[7].append(lambda: fint(even_next, "g"))
+                    plan[(1, 3, 9, 11)[k] if more else 5 + 2 * (k // 2)].append(lambda k=k: fold(g - 1, k))
+            for k in range(4):
+                plan[late + 1 + 2 * (k // 2)].append(lambda k=k: f2_tile(odd, k))
+            plan[qf_odd].append(lambda: quant_f(odd))
+            if more:
+                plan[qf_odd].append(lambda: hreg(o, "g"))
                 for k in range(4):
-                    plan[9 + 2 * (k // 2)].append(lambda k=k: f2_tile(even_next, k))
-                plan[10].append(lambda: quant_h(odd_next))
+                    plan[late + 5 + 2 * (k // 2)].append(lambda k=k: st1(e, k))
+                plan[qh_o].append(lambda: quant_h(o))
+                plan[qh_o].append(lambda: fint(e, "g"))
                 for k in range(4):
-                    plan[13 + 2 * (k // 2)].append(lambda k=k: st1(odd_next, k))
-                plan[14].append(lambda: quant_f(even_next))
-                if odd_next + 1 < NCHUNK:
-                    plan[14].append(lambda: hreg(odd_next + 1, "g"))
-                plan[15].append(lambda: fint(odd_next, "g"))
+                    plan[late + 9 + 2 * (k // 2)].append(lambda k=k: f2_tile(e, k))
+                plan[qf_e].append(lambda: quant_f(e))
                 for k in range(4):
-                    plan[17 + 2 * k].append(lambda k=k: first(g + 1, k))
-                if odd_next + 1 < NCHUNK:
-                    plan[18].append(lambda: quant_h(odd_next + 1))
-                plan[22].append(lambda: quant_f(odd_next))
-            if g > 0:
-                for pc in range(NPC):
-                    tile2(g, 1, pc)
-            for k in range(0 if g > 0 else 4, 24 if g + 1 < NG else 8):
-                tile2(g, 2 + k // 4, k % 4)
+                    plan[late + 13 + 2 * (k // 2)].append(lambda k=k: st1(o, k))
+                if e + 2 < NCHUNK:
+                    plan[qf_e].append(lambda: hreg(e + 2, "g"))
+                    plan[qh_ne].append(lambda: quant_h(e + 2))
+                plan[qh_ne].append(lambda: fint(o, "g"))
+                for k in range(4):
+                    plan[(21, 23, 25, 27)[k]].append(lambda k=k: (pair if k < 0 else first)(g + 1, k))
+            for k in range(28 if more else 12):
+                if g == 0 or k >= 0:
+                    tile2(g, 1 + k // 4, k % 4)
                 for f in plan[k]:
                     f()
 

@@ -38,6 +38,9 @@ def tile_protopnet_pa_kernel(tc, h_relu, conv2_w, conv2_b, prototypes, out):
         work = ctx.enter_context(tc.tile_pool(name="work", bufs=2))
         psum = ctx.enter_context(tc.psum_pool(name="psum", bufs=2))
 
+        warm = const.tile([P, 512], BF16)
+        nc.vector.memset(warm[:], 0.0)
+
         w_sb = const.tile([P, 4, CH], BF16)
         nc.sync.dma_start(out=w_sb[:], in_=conv2_w.rearrange("(q t) c -> q t c", t=4))
         b_bf = const.tile([P, 4], BF16)
@@ -79,6 +82,11 @@ def tile_protopnet_pa_kernel(tc, h_relu, conv2_w, conv2_b, prototypes, out):
         junk = const.tile([P, CH], BF16)
         junk32 = const.tile([P, CH], BF16)
         best = const.tile([P, NIMG * 16], F32)
+
+        def keep_warm(n):
+            for k in range(n):
+                idle = psum.tile([P, 512], F32, name="aux", bufs=4)
+                nc.tensor.matmul(out=idle[:], lhsT=warm[:, :P], rhs=warm[:], start=True, stop=True)
 
         def words_transpose(src, first_tile):
             banks = []
@@ -257,7 +265,9 @@ def tile_protopnet_pa_kernel(tc, h_relu, conv2_w, conv2_b, prototypes, out):
             nc.scalar.activation(out=junk[:], in_=proto_sb[:, rt, :], func=ACT.Square,
                                  accum_out=p2_sb[:, rt:rt + 1])
 
+        keep_warm(10)
         wb = words_transpose(w_sb, 0)
+        keep_warm(5)
         wg = words_copy(wb, "s")
         hreg(0, "v", [0, 1])
         hreg(0, "v", [2, 3])

@@ -265,15 +265,16 @@ def tile_protopnet_pa_kernel(tc, h_relu, conv2_w, conv2_b, prototypes, out):
             nc.scalar.activation(out=junk[:], in_=proto_sb[:, rt, :], func=ACT.Square,
                                  accum_out=p2_sb[:, rt:rt + 1])
 
-        keep_warm(10)
-        wb = words_transpose(w_sb, 0)
         keep_warm(5)
+        wb = words_transpose(w_sb, 0)
+        keep_warm(4)
         wg = words_copy(wb, "s")
         hreg(0, "v", [0, 1])
         hreg(0, "v", [2, 3])
         words_quant(wg, wcodes[:], wscales[:])
         quant_h(0)
         pb = words_transpose(proto_sb, 0)
+        keep_warm(2)
         pg0 = words_copy(pb, "s")
         hreg(1, "v")
         pb = words_transpose(proto_sb, 4)
@@ -283,20 +284,20 @@ def tile_protopnet_pa_kernel(tc, h_relu, conv2_w, conv2_b, prototypes, out):
         quant_h(1)
         words_quant(pg0, *proto_cols(0))
         words_quant(pg1, *proto_cols(1))
-        fint(0, "v")
         pb = words_transpose(proto_sb, 8)
         pg2 = words_copy(pb, "v")
-        quant_f(0)
+        fint(0, "v")
         words_quant(pg2, *proto_cols(2))
+        quant_f(0)
         for jl in range(4):
             f2_tile(0, jl)
         pb = words_transpose(proto_sb, 12)
         pg3 = words_copy(pb, "v", gp_tile())
-        for pc in range(NPC):
-            first(0, pc)
-            if pc == 0:
-                words_quant(pg3, *proto_cols(3))
-                hreg(2, "g")
+        first(0, 0)
+        first(0, 1)
+        first(0, 2)
+        words_quant(pg3, *proto_cols(3))
+        hreg(2, "g")
 
         for g in range(NG):
             plan = [[] for k in range(28)]
@@ -305,6 +306,7 @@ def tile_protopnet_pa_kernel(tc, h_relu, conv2_w, conv2_b, prototypes, out):
             o = odd + 2
             more = g + 1 < NG
             if g == 0:
+                plan[0].append(lambda: first(0, 3))
                 for k in range(4):
                     plan[0 + k].append(lambda k=k: st1(1, k))
                 plan[5].append(lambda: quant_h(2))

@@ -128,11 +128,11 @@ def tile_protopnet_pa_kernel(tc, h_relu, conv2_w, conv2_b, prototypes, out):
         fcodes = [None] * NCHUNK
         fscales = [None] * NCHUNK
         ng_sb = [None] * NCHUNK
-        dng_sb = [None] * NCHUNK
+        dng_sb = [[] for m in range(NCHUNK)]
         rmax = [[None] * NPC for g in range(NG)]
 
         def gp_tile():
-            return work.tile([P, 5 * CW], BF16, name="gp_out", bufs=1, align_bytes=64)
+            return work.tile([P, 6 * CW], BF16, name="gp_out", bufs=1, align_bytes=64)
 
         def hreg(m, eng, images=range(GI)):
             g = m // 2
@@ -180,13 +180,13 @@ def tile_protopnet_pa_kernel(tc, h_relu, conv2_w, conv2_b, prototypes, out):
             if jl == 3:
                 ng_sb[m] = work.tile([P, 4], F32, name="ng_sb", bufs=4)
                 nc.scalar.mul(out=ng_sb[m][:], in_=f2c[m][:], mul=-0.5)
-                if paired(m):
-                    dng_sb[m] = work.tile([P, 1], F32, name="dng_sb", bufs=2)
-                    nc.scalar.activation(out=dng_sb[m][:], in_=f2c[m][:, 1:2], func=ACT.Identity,
-                                         bias=ng_sb[m][:, 0:1], scale=0.5)
+                for i, jn in enumerate(negated(m)):
+                    dng_sb[m].append(work.tile([P, 1], F32, name="dng_sb", bufs=3))
+                    nc.scalar.activation(out=dng_sb[m][i][:], in_=f2c[m][:, jn:jn + 1], func=ACT.Identity,
+                                         bias=ng_sb[m][:, jn - 1:jn], scale=0.5)
 
-        def paired(m):
-            return False
+        def negated(m):
+            return [1, 3] if m == NCHUNK - 1 else []
 
         def fint(m, eng):
             if eng == "v":
@@ -198,23 +198,25 @@ def tile_protopnet_pa_kernel(tc, h_relu, conv2_w, conv2_b, prototypes, out):
             if eng == "v":
                 nc.vector.tensor_copy(out=dst, in_=src)
             else:
+                for i, jn in enumerate(negated(m)):
+                    nc.gpsimd.tensor_scalar(
+                        out=fgc[m][:, (4 + i) * CW:(5 + i) * CW].rearrange("p (c t) -> p c t", t=4),
+                        in0=f32c[m][:, :, jn * P:(jn + 1) * P].rearrange("p t c -> p c t"),
+                        scalar1=-1.0, scalar2=0.0, op0=ALU.mult, op1=ALU.add)
                 nc.gpsimd.tensor_scalar(out=dst, in0=src, scalar1=1.0, scalar2=0.0,
                                         op0=ALU.mult, op1=ALU.add)
-                if paired(m):
-                    nc.gpsimd.tensor_scalar(
-                        out=fgc[m][:, 4 * CW:].rearrange("p (c t) -> p c t", t=4),
-                        in0=f32c[m][:, :, P:2 * P].rearrange("p t c -> p c t"),
-                        scalar1=-1.0, scalar2=0.0, op0=ALU.mult, op1=ALU.add)
 
         def quant_f(m):
-            width = CW + P
+            width = CW + 2 * P
             fcodes[m] = work.tile([P, width], U32, name="fcodes", bufs=4, align_bytes=64)
             fscales[m] = work.tile([P, width], U8, name="fscales", bufs=4, align_bytes=64)
             nc.vector.quantize_mx(out=fcodes[m][:, :CW].bitcast(FP8X4), scales=fscales[m][:, :CW],
                                   in_=fgc[m][:, :4 * CW])
-            if paired(m):
-                nc.vector.quantize_mx(out=fcodes[m][:, CW:].bitcast(FP8X4), scales=fscales[m][:, CW:],
-                                      in_=fgc[m][:, 4 * CW:])
+            n = len(negated(m))
+            if n > 0:
+                nc.vector.quantize_mx(out=fcodes[m][:, CW:CW + n * P].bitcast(FP8X4),
+                                      scales=fscales[m][:, CW:CW + n * P],
+                                      in_=fgc[m][:, 4 * CW:(4 + n) * CW])
 
         def fp_pass(x, m, jl, pc, start=True, stop=True):
             nc.tensor.matmul_mx(out=x[:], lhsT=fcodes[m][:, jl * P:(jl + 1) * P].bitcast(FP8X4),
@@ -230,19 +232,28 @@ def tile_protopnet_pa_kernel(tc, h_relu, conv2_w, conv2_b, prototypes, out):
             nc.scalar.activation(out=rmax[g][pc][:], in_=x[:], func=ACT.Identity,
                                  bias=ng_sb[2 * g][:, 0:1], scale=1.0)
 
-        def pair(g, pc):
-            m = 2 * g
+        def pair(m, jl, pc, sums):
+            i = negated(m).index(jl + 1)
             xd = psum.tile([P, 512], F32, name="aux", bufs=4)
-            fp_pass(xd, m, 0, pc, start=True, stop=False)
-            fp_pass(xd, m, 4, pc, start=False, stop=True)
+            fp_pass(xd, m, jl, pc, start=True, stop=False)
+            fp_pass(xd, m, 4 + i, pc, start=False, stop=True)
             dd = work.tile([P, 512], F32, name="dd", bufs=4)
-            nc.scalar.activation(out=dd[:], in_=xd[:], func=ACT.Relu, bias=dng_sb[m][:], scale=1.0)
+            nc.scalar.activation(out=dd[:], in_=xd[:], func=ACT.Relu, bias=dng_sb[m][i][:], scale=1.0)
             xb = psum.tile([P, 512], F32, name="aux", bufs=4)
-            fp_pass(xb, m, 1, pc)
-            rmax[g][pc] = work.tile([P, 512], F32, name="rmax%d" % pc, bufs=3)
-            nc.scalar.activation(out=rmax[g][pc][:], in_=xb[:], func=ACT.Identity,
-                                 bias=ng_sb[m][:, 1:2], scale=1.0)
-            nc.gpsimd.tensor_tensor(out=rmax[g][pc][:], in0=rmax[g][pc][:], in1=dd[:], op=ALU.add)
+            fp_pass(xb, m, jl + 1, pc)
+            nc.scalar.activation(out=sums[:], in_=xb[:], func=ACT.Identity,
+                                 bias=ng_sb[m][:, jl + 1:jl + 2], scale=1.0)
+            nc.gpsimd.tensor_tensor(out=sums[:], in0=sums[:], in1=dd[:], op=ALU.add)
+
+        joined = {}
+
+        def late_pair(jl, pc):
+            joined[jl, pc] = work.tile([P, 512], F32, name="joined", bufs=8)
+            pair(NCHUNK - 1, jl, pc, joined[jl, pc])
+
+        def merge(jl, pc):
+            r = rmax[NG - 1][pc]
+            nc.vector.tensor_tensor(out=r[:], in0=r[:], in1=joined[jl, pc][:], op=ALU.max)
 
         def tile2(g, j, pc):
             m = 2 * g + j // 4
@@ -260,10 +271,6 @@ def tile_protopnet_pa_kernel(tc, h_relu, conv2_w, conv2_b, prototypes, out):
             nc.vector.tensor_reduce(out=bview[:, 4 * pc:4 * pc + 4, GI * g:GI * (g + 1)],
                                     in_=bank[:].rearrange("p a (i r) -> p a i r", i=GI),
                                     axis=AX.X, op=ALU.max)
-
-        def p2_part(rt):
-            nc.scalar.activation(out=junk[:], in_=proto_sb[:, rt, :], func=ACT.Square,
-                                 accum_out=p2_sb[:, rt:rt + 1])
 
         keep_warm(5)
         wb = words_transpose(w_sb, 0)
@@ -299,62 +306,93 @@ def tile_protopnet_pa_kernel(tc, h_relu, conv2_w, conv2_b, prototypes, out):
         words_quant(pg3, *proto_cols(3))
         hreg(2, "g")
 
-        for g in range(NG):
+        p2_next = [0]
+
+        def p2_part():
+            rt = p2_next[0]
+            p2_next[0] = rt + 1
+            nc.scalar.activation(out=junk[:], in_=proto_sb[:, rt, :], func=ACT.Square,
+                                 accum_out=p2_sb[:, rt:rt + 1])
+
+        def at(plan, places, work_of):
+            for k, place in enumerate(places):
+                plan[place].append(lambda k=k: work_of(k))
+
+        last = NG - 1
+        pairs = [(0, 0), (0, 1), (0, 2), (0, 3), (2, 3), (2, 2), (2, 1), (2, 0)][:8]
+        for g in range(NG - 1):
             plan = [[] for k in range(28)]
             odd = 2 * g + 1
             e = odd + 1
             o = odd + 2
-            more = g + 1 < NG
+            late = 0
             if g == 0:
+                qf_odd, qh_o, qf_e, qh_ne = 10, 15, 20, 25
+                late = 4
                 plan[0].append(lambda: first(0, 3))
-                for k in range(4):
-                    plan[0 + k].append(lambda k=k: st1(1, k))
+                at(plan, [0, 1, 2, 3], lambda k: st1(1, k))
+                at(plan, [16, 17, 18, 19, 20], lambda k: p2_part())
                 plan[5].append(lambda: quant_h(2))
                 plan[5].append(lambda: fint(1, "g"))
-                qf_odd, qh_o, qf_e, qh_ne, late = 10, 15, 20, 25, 4
+            elif g == 1:
+                qf_odd, qh_o, qf_e, qh_ne = 3, 10, 16, 22
+                at(plan, [16, 17, 18, 19, 20, 22, 24, 26], lambda k: p2_part())
             else:
-                qf_odd, qh_o, qf_e, qh_ne, late = 3, 10, 16, 22, 0
-                for k in range(4):
-                    plan[(1, 3, 9, 11)[k] if more else 5 + 2 * (k // 2)].append(lambda k=k: fold(g - 1, k))
-            for k in range(4):
-                plan[late + 1 + 2 * (k // 2)].append(lambda k=k: f2_tile(odd, k))
+                qf_odd, qh_o, qf_e, qf_o = 3, 10, 16, 25
+            if g > 0:
+                at(plan, [1, 3, 9, 11] if g == 1 else [1, 3, 9, 11], lambda k: fold(g - 1, k))
+            at(plan, [late + k for k in (1, 1, 1+2, 1+2)], lambda k: f2_tile(odd, k))
             plan[qf_odd].append(lambda: quant_f(odd))
-            if more:
-                plan[qf_odd].append(lambda: hreg(o, "g"))
-                for k in range(4):
-                    plan[late + 5 + 2 * (k // 2)].append(lambda k=k: st1(e, k))
-                plan[qh_o].append(lambda: quant_h(o))
-                plan[qh_o].append(lambda: fint(e, "g"))
-                for k in range(4):
-                    plan[late + 9 + 2 * (k // 2)].append(lambda k=k: f2_tile(e, k))
-                plan[qf_e].append(lambda: quant_f(e))
-                for k in range(4):
-                    plan[late + 13 + 2 * (k // 2)].append(lambda k=k: st1(o, k))
-                if e + 2 < NCHUNK:
-                    plan[qf_e].append(lambda: hreg(e + 2, "g"))
-                    plan[qh_ne].append(lambda: quant_h(e + 2))
+            plan[qf_odd].append(lambda: hreg(o, "g"))
+            at(plan, [late + k for k in (5, 5, 5+2, 5+2)], lambda k: st1(e, k))
+            plan[qh_o].append(lambda: quant_h(o))
+            plan[qh_o].append(lambda: fint(e, "g"))
+            at(plan, [late + k for k in (9, 9, 9+2, 9+2)], lambda k: f2_tile(e, k))
+            plan[qf_e].append(lambda: quant_f(e))
+            if g + 2 < NG:
+                plan[qf_e].append(lambda: hreg(e + 2, "g"))
+                plan[qh_ne].append(lambda: quant_h(e + 2))
+                at(plan, [21, 23, 25, 27], lambda k: first(g + 1, k))
+                at(plan, [late + k for k in (13, 13, 15, 15)], lambda k: st1(o, k))
                 plan[qh_ne].append(lambda: fint(o, "g"))
-                for k in range(4):
-                    plan[(21, 23, 25, 27)[k]].append(lambda k=k: (pair if k < 0 else first)(g + 1, k))
-            for k in range(28 if more else 12):
-                if g == 0 or k >= 0:
-                    tile2(g, 1 + k // 4, k % 4)
+            else:
+                at(plan, [13, 13, 15, 15], lambda k: st1(o, k))
+                plan[qf_e].append(lambda: fint(o, "g"))
+                at(plan, [18, 18, 20, 20], lambda k: f2_tile(o, k))
+                at(plan, [20, 22, 24], lambda k: p2_part())
+                plan[qf_o].append(lambda: quant_f(o))
+                at(plan, [21, 23, 25, 27], lambda k: first(g + 1, k))
+                at(plan, [], lambda k: late_pair(*pairs[k]))
+            for k in range(28):
+                tile2(g, 1 + k // 4, k % 4)
                 for f in plan[k]:
                     f()
 
-        last = NG - 1
-        for j in range(4, NJ):
-            tile2(last, j, 0)
-            tile2(last, j, 1)
-            for k in range(4):
-                p2_part(4 * (j - 4) + k)
-        for j in range(4, NJ):
-            tile2(last, j, 2)
-            tile2(last, j, 3)
-            if j < 6:
-                fold(last, j - 4)
-        fold(last, 2)
-        fold(last, 3)
+        units = [lambda pc=pc: tile2(last, 1, pc) for pc in range(NPC)]
+        units += [lambda pc=pc: tile2(last, 2, pc) for pc in range(NPC)]
+        units += [lambda pc=pc: fold(last - 1, pc) for pc in range(NPC)]
+        units += [lambda pc=pc: tile2(last, 3, pc) for pc in range(NPC)]
+        for jl in (0, 2):
+            units += [lambda j=j, pc=pc: tile2(last, j, pc) for j in (4 + jl, 5 + jl) for pc in range(NPC)
+                      if (jl, pc) not in pairs]
+        done = 0
+        for k, unit in enumerate(units):
+            unit()
+            if k >= 1 and (k - 1) % 3 == 0 and done < len(pairs):
+                late_pair(*pairs[done])
+                done += 1
+        for k in range(done, len(pairs)):
+            late_pair(*pairs[k])
+        for k in range(16 - p2_next[0]):
+            p2_part()
+        for pc in range(NPC):
+            merge(0, pc)
+        for k in range(NPC):
+            if (2, NPC - 1 - k) in pairs:
+                merge(2, NPC - 1 - k)
+            if k > 0:
+                fold(last, NPC - k)
+        fold(last, 0)
 
         for half in range(2):
             res = const.tile([P, P], F32, name="res%d" % half)

@@ -319,7 +319,7 @@ def tile_protopnet_pa_kernel(tc, h_relu, conv2_w, conv2_b, prototypes, out):
                 plan[place].append(lambda k=k: work_of(k))
 
         last = NG - 1
-        pairs = [(0, 0), (0, 1), (0, 2), (0, 3), (2, 3), (2, 2), (2, 1), (2, 0)][:8]
+        pairs = [(0, 0), (0, 1), (0, 2), (0, 3), (2, 3), (2, 2), (2, 1), (2, 0)][:4]
         for g in range(NG - 1):
             plan = [[] for k in range(28)]
             odd = 2 * g + 1
@@ -327,13 +327,12 @@ def tile_protopnet_pa_kernel(tc, h_relu, conv2_w, conv2_b, prototypes, out):
             o = odd + 2
             late = 0
             if g == 0:
-                qf_odd, qh_o, qf_e, qh_ne = 10, 15, 20, 25
-                late = 4
+                qf_odd, qh_o, qf_e, qh_ne = 9, 14, 19, 26
                 plan[0].append(lambda: first(0, 3))
                 at(plan, [0, 1, 2, 3], lambda k: st1(1, k))
                 at(plan, [16, 17, 18, 19, 20], lambda k: p2_part())
-                plan[5].append(lambda: quant_h(2))
-                plan[5].append(lambda: fint(1, "g"))
+                plan[4].append(lambda: quant_h(2))
+                plan[4].append(lambda: fint(1, "g"))
             elif g == 1:
                 qf_odd, qh_o, qf_e, qh_ne = 3, 10, 16, 22
                 at(plan, [16, 17, 18, 19, 20, 22, 24, 26], lambda k: p2_part())
@@ -341,19 +340,19 @@ def tile_protopnet_pa_kernel(tc, h_relu, conv2_w, conv2_b, prototypes, out):
                 qf_odd, qh_o, qf_e, qf_o = 3, 10, 16, 25
             if g > 0:
                 at(plan, [1, 3, 9, 11] if g == 1 else [1, 3, 9, 11], lambda k: fold(g - 1, k))
-            at(plan, [late + k for k in (1, 1, 1+2, 1+2)], lambda k: f2_tile(odd, k))
+            at(plan, [5, 5, 7, 7] if g == 0 else [1, 1, 3, 3], lambda k: f2_tile(odd, k))
             plan[qf_odd].append(lambda: quant_f(odd))
             plan[qf_odd].append(lambda: hreg(o, "g"))
-            at(plan, [late + k for k in (5, 5, 5+2, 5+2)], lambda k: st1(e, k))
+            at(plan, [9, 9, 11, 11] if g == 0 else [5, 5, 7, 7], lambda k: st1(e, k))
             plan[qh_o].append(lambda: quant_h(o))
             plan[qh_o].append(lambda: fint(e, "g"))
-            at(plan, [late + k for k in (9, 9, 9+2, 9+2)], lambda k: f2_tile(e, k))
+            at(plan, [13, 13, 15, 15] if g == 0 else [9, 9, 11, 11], lambda k: f2_tile(e, k))
             plan[qf_e].append(lambda: quant_f(e))
             if g + 2 < NG:
                 plan[qf_e].append(lambda: hreg(e + 2, "g"))
                 plan[qh_ne].append(lambda: quant_h(e + 2))
-                at(plan, [21, 23, 25, 27], lambda k: first(g + 1, k))
-                at(plan, [late + k for k in (13, 13, 15, 15)], lambda k: st1(o, k))
+                at(plan, [21, 23, 25, 27] if g == 0 else [21, 23, 25, 27], lambda k: first(g + 1, k))
+                at(plan, [17, 17, 19, 19] if g == 0 else [13, 13, 15, 15], lambda k: st1(o, k))
                 plan[qh_ne].append(lambda: fint(o, "g"))
             else:
                 at(plan, [13, 13, 15, 15], lambda k: st1(o, k))
@@ -372,27 +371,29 @@ def tile_protopnet_pa_kernel(tc, h_relu, conv2_w, conv2_b, prototypes, out):
         units += [lambda pc=pc: tile2(last, 2, pc) for pc in range(NPC)]
         units += [lambda pc=pc: fold(last - 1, pc) for pc in range(NPC)]
         units += [lambda pc=pc: tile2(last, 3, pc) for pc in range(NPC)]
-        for jl in (0, 2):
-            units += [lambda j=j, pc=pc: tile2(last, j, pc) for j in (4 + jl, 5 + jl) for pc in range(NPC)
-                      if (jl, pc) not in pairs]
+        ends = []
+        for half in ((0, 1), (2, 3)):
+            alone = [pc for pc in half if (2, pc) not in pairs]
+            ends += [lambda j=j, pc=pc: tile2(last, j, pc) for j in (6, 7) for pc in alone]
+            ends += [lambda jl=jl, pc=pc: merge(jl, pc) for jl in (0, 2) for pc in half if (jl, pc) in pairs]
+            if half == (0, 1):
+                first_half = len(ends)
+        ends.insert(first_half + 1, lambda: fold(last, 0))
+        ends.insert(first_half + 3, lambda: fold(last, 1))
         done = 0
-        for k, unit in enumerate(units):
+        for k, unit in enumerate(units + ends[:4]):
             unit()
-            if k >= 1 and (k - 1) % 3 == 0 and done < len(pairs):
+            if k >= 1 and (k - 1) % 4 == 0 and done < len(pairs):
                 late_pair(*pairs[done])
                 done += 1
         for k in range(done, len(pairs)):
             late_pair(*pairs[k])
         for k in range(16 - p2_next[0]):
             p2_part()
-        for pc in range(NPC):
-            merge(0, pc)
-        for k in range(NPC):
-            if (2, NPC - 1 - k) in pairs:
-                merge(2, NPC - 1 - k)
-            if k > 0:
-                fold(last, NPC - k)
-        fold(last, 0)
+        for end in ends[4:]:
+            end()
+        fold(last, 2)
+        fold(last, 3)
 
         for half in range(2):
             res = const.tile([P, P], F32, name="res%d" % half)

@@ -38,9 +38,6 @@ def tile_protopnet_pa_kernel(tc, h_relu, conv2_w, conv2_b, prototypes, out):
         work = ctx.enter_context(tc.tile_pool(name="work", bufs=2))
         psum = ctx.enter_context(tc.psum_pool(name="psum", bufs=2))
 
-        warm = const.tile([P, 512], BF16)
-        nc.vector.memset(warm[:], 0.0)
-
         w_sb = const.tile([P, 4, CH], BF16)
         nc.sync.dma_start(out=w_sb[:], in_=conv2_w.rearrange("(q t) c -> q t c", t=4))
         b_bf = const.tile([P, 4], BF16)
@@ -82,11 +79,6 @@ def tile_protopnet_pa_kernel(tc, h_relu, conv2_w, conv2_b, prototypes, out):
         junk = const.tile([P, CH], BF16)
         junk32 = const.tile([P, CH], BF16)
         best = const.tile([P, NIMG * 16], F32)
-
-        def keep_warm(n):
-            for k in range(n):
-                idle = psum.tile([P, 512], F32, name="aux", bufs=4)
-                nc.tensor.matmul(out=idle[:], lhsT=warm[:, :P], rhs=warm[:], start=True, stop=True)
 
         def words_transpose(src, first_tile):
             banks = []
@@ -186,7 +178,7 @@ def tile_protopnet_pa_kernel(tc, h_relu, conv2_w, conv2_b, prototypes, out):
                                          bias=ng_sb[m][:, jn - 1:jn], scale=0.5)
 
         def negated(m):
-            return [1, 3] if m == NCHUNK - 1 else []
+            return [1] if m == NCHUNK - 1 else []
 
         def fint(m, eng):
             if eng == "v":
@@ -272,16 +264,13 @@ def tile_protopnet_pa_kernel(tc, h_relu, conv2_w, conv2_b, prototypes, out):
                                     in_=bank[:].rearrange("p a (i r) -> p a i r", i=GI),
                                     axis=AX.X, op=ALU.max)
 
-        keep_warm(5)
         wb = words_transpose(w_sb, 0)
-        keep_warm(4)
         wg = words_copy(wb, "s")
         hreg(0, "v", [0, 1])
         hreg(0, "v", [2, 3])
         words_quant(wg, wcodes[:], wscales[:])
         quant_h(0)
         pb = words_transpose(proto_sb, 0)
-        keep_warm(2)
         pg0 = words_copy(pb, "s")
         hreg(1, "v")
         pb = words_transpose(proto_sb, 4)

@@ -22,18 +22,23 @@ NG = NIMG // GI
 RPOS = P // GI
 NJ = HW // RPOS
 CW = 512
+TC = CW // P
 NCHUNK = NIMG * HW // CW
-NPC = NPROTO // 512
+PW = 512
+NPC = NPROTO // PW
+NPT = NPROTO // P
+LAST = NG - 1
+LAST_CHUNK = NCHUNK - 1
+
+APART_COLS = (2, 3)
 
 FLOPS = 2 * CH * CH * NIMG * HW + 2 * NPROTO * CH * NIMG * HW
-MANUAL = True
 
 
 def tile_protopnet_pa_kernel(tc, h_relu, conv2_w, conv2_b, prototypes, out):
     nc = tc.nc
     with ExitStack() as ctx:
-        if MANUAL:
-            ctx.enter_context(tc.manual_schedule())
+        ctx.enter_context(tc.manual_schedule())
         const = ctx.enter_context(tc.tile_pool(name="const", bufs=1))
         work = ctx.enter_context(tc.tile_pool(name="work", bufs=2))
         psum = ctx.enter_context(tc.psum_pool(name="psum", bufs=2))
@@ -43,7 +48,7 @@ def tile_protopnet_pa_kernel(tc, h_relu, conv2_w, conv2_b, prototypes, out):
         b_bf = const.tile([P, 4], BF16)
         nc.scalar.dma_start(out=b_bf[:], in_=conv2_b.rearrange("(q t) -> q t", t=4))
         h_sb = [None] * NG
-        proto_sb = const.tile([P, 16, CH], BF16)
+        proto_sb = const.tile([P, NPT, CH], BF16)
 
         def load_h(g, pieces):
             h_sb[g] = work.tile([P, GI, 4 * HW], BF16, name="h_sb", bufs=NG)
@@ -57,10 +62,10 @@ def tile_protopnet_pa_kernel(tc, h_relu, conv2_w, conv2_b, prototypes, out):
         def load_proto(pc):
             nc.sync.dma_start(
                 out=proto_sb[:, 4 * pc:4 * pc + 4, :],
-                in_=prototypes[pc * 512:(pc + 1) * 512, :].rearrange("(a r) d -> r a d", r=P),
+                in_=prototypes[pc * PW:(pc + 1) * PW, :].rearrange("(a r) d -> r a d", r=P),
             )
 
-        load_h(0, 2)
+        load_h(0, GI)
         for pc in range(NPC):
             load_proto(pc)
         for g in range(1, NG):
@@ -75,10 +80,11 @@ def tile_protopnet_pa_kernel(tc, h_relu, conv2_w, conv2_b, prototypes, out):
         wscales = const.tile([P, CH], U8, align_bytes=64)
         pcodes = const.tile([P, NPROTO], U32, align_bytes=64)
         pscales = const.tile([P, NPROTO], U8, align_bytes=64)
-        p2_sb = const.tile([P, 16], F32)
+        p2_sb = const.tile([P, NPT], F32)
         junk = const.tile([P, CH], BF16)
         junk32 = const.tile([P, CH], BF16)
-        best = const.tile([P, NIMG * 16], F32)
+        best = const.tile([P, NIMG * NPT], F32)
+        best67 = const.tile([P, GI * NPT], F32)
 
         def words_transpose(src, first_tile):
             banks = []
@@ -92,11 +98,11 @@ def tile_protopnet_pa_kernel(tc, h_relu, conv2_w, conv2_b, prototypes, out):
                 banks.append(bank)
             return banks
 
-        def words_copy(banks, eng, grouped=None):
+        def words_copy(banks, eng, grouped=None, halves=(0, 1)):
             if grouped is None:
-                grouped = work.tile([P, 4 * 512], BF16, name="grouped", align_bytes=64)
-            gw = grouped[:, :4 * 512].bitcast(F32)
-            for half in range(2):
+                grouped = work.tile([P, 4 * PW], BF16, name="grouped", align_bytes=64)
+            gw = grouped[:, :4 * PW].bitcast(F32)
+            for half in halves:
                 dst = gw[:, half * 512:(half + 1) * 512].rearrange("q (a r u) -> q a r u", a=2, u=2)
                 src = banks[half][:].rearrange("q a u r -> q a r u")
                 if eng == "v":
@@ -106,10 +112,10 @@ def tile_protopnet_pa_kernel(tc, h_relu, conv2_w, conv2_b, prototypes, out):
             return grouped
 
         def words_quant(grouped, codes, scales):
-            nc.vector.quantize_mx(out=codes.bitcast(FP8X4), scales=scales, in_=grouped[:, :4 * 512])
+            nc.vector.quantize_mx(out=codes.bitcast(FP8X4), scales=scales, in_=grouped[:, :4 * PW])
 
         def proto_cols(pc):
-            return pcodes[:, pc * 512:(pc + 1) * 512], pscales[:, pc * 512:(pc + 1) * 512]
+            return pcodes[:, pc * PW:(pc + 1) * PW], pscales[:, pc * PW:(pc + 1) * PW]
 
         hg = [None] * NCHUNK
         hcodes = [None] * NCHUNK
@@ -128,22 +134,22 @@ def tile_protopnet_pa_kernel(tc, h_relu, conv2_w, conv2_b, prototypes, out):
 
         def hreg(m, eng, images=range(GI)):
             g = m // 2
-            j0 = 4 * (m % 2)
+            j0 = TC * (m % 2)
             if hg[m] is None:
                 if eng == "g":
                     hg[m] = gp_tile()
                 else:
-                    hg[m] = work.tile([P, 4 * CW], BF16, name="hg_" + eng, bufs=1, align_bytes=64)
-            dst = hg[m][:, :4 * CW].rearrange("p (j i r c) -> p i j r c", j=4, i=GI, c=4)
-            for i in images:
-                src = h_sb[g][:, i, :].rearrange("p (c j r) -> p j r c", c=4, j=NJ)[:, j0:j0 + 4]
-                if eng == "v":
-                    nc.vector.tensor_copy(out=dst[:, i], in_=src)
-                elif eng == "s":
-                    nc.scalar.copy(out=dst[:, i], in_=src)
-                else:
-                    nc.gpsimd.tensor_scalar(out=dst[:, i], in0=src, scalar1=1.0,
-                                            scalar2=0.0, op0=ALU.mult, op1=ALU.add)
+                    hg[m] = work.tile([P, 4 * CW], BF16, name="hg%d" % m, bufs=1, align_bytes=64)
+            dst = hg[m][:, :4 * CW].rearrange("p (j i r c) -> p i j r c", j=TC, i=GI, c=4)
+            src = h_sb[g][:].rearrange("p i (c j r) -> p i j r c", c=4, j=NJ)[:, :, j0:j0 + TC]
+            if eng == "g":
+                nc.gpsimd.tensor_scalar(out=dst, in0=src, scalar1=1.0, scalar2=0.0, op0=ALU.mult, op1=ALU.add)
+            else:
+                for i in images:
+                    if eng == "v":
+                        nc.vector.tensor_copy(out=dst[:, i], in_=src[:, i])
+                    else:
+                        nc.scalar.copy(out=dst[:, i], in_=src[:, i])
 
         def quant_h(m):
             hcodes[m] = work.tile([P, CW], U32, name="hcodes", bufs=4, align_bytes=64)
@@ -161,24 +167,24 @@ def tile_protopnet_pa_kernel(tc, h_relu, conv2_w, conv2_b, prototypes, out):
             nc.scalar.activation(out=f32c[m][:, t, :], in_=z[:], func=ACT.Sigmoid,
                                  bias=b_f32[:, t:t + 1], scale=1.0)
 
+        def negated(m):
+            return [1, 3] if m == LAST_CHUNK else []
+
         def f2_tile(m, jl):
             if jl == 0:
-                f2c[m] = work.tile([P, 4], F32, name="f2c", bufs=4)
+                f2c[m] = work.tile([P, TC], F32, name="f2c", bufs=4)
             bank = psum.tile([P, 4, P], F32, name="aux", bufs=4)
             for t in range(4):
                 nc.tensor.transpose(bank[:, t, :], f32c[m][:, t, jl * P:(jl + 1) * P], ident[:])
             nc.scalar.activation(out=junk32[:], in_=bank[:].rearrange("p t q -> p (t q)"), func=ACT.Square,
                                  accum_out=f2c[m][:, jl:jl + 1])
-            if jl == 3:
-                ng_sb[m] = work.tile([P, 4], F32, name="ng_sb", bufs=4)
+            if jl == TC - 1:
+                ng_sb[m] = work.tile([P, TC], F32, name="ng_sb", bufs=4)
                 nc.scalar.mul(out=ng_sb[m][:], in_=f2c[m][:], mul=-0.5)
                 for i, jn in enumerate(negated(m)):
                     dng_sb[m].append(work.tile([P, 1], F32, name="dng_sb", bufs=3))
                     nc.scalar.activation(out=dng_sb[m][i][:], in_=f2c[m][:, jn:jn + 1], func=ACT.Identity,
                                          bias=ng_sb[m][:, jn - 1:jn], scale=0.5)
-
-        def negated(m):
-            return [1] if m == NCHUNK - 1 else []
 
         def fint(m, eng):
             if eng == "v":
@@ -213,44 +219,21 @@ def tile_protopnet_pa_kernel(tc, h_relu, conv2_w, conv2_b, prototypes, out):
         def fp_pass(x, m, jl, pc, start=True, stop=True):
             nc.tensor.matmul_mx(out=x[:], lhsT=fcodes[m][:, jl * P:(jl + 1) * P].bitcast(FP8X4),
                                 lhsT_scale=fscales[m][:, jl * P:(jl + 1) * P],
-                                rhs=pcodes[:, pc * 512:(pc + 1) * 512].bitcast(FP8X4),
-                                rhs_scale=pscales[:, pc * 512:(pc + 1) * 512],
+                                rhs=pcodes[:, pc * PW:(pc + 1) * PW].bitcast(FP8X4),
+                                rhs_scale=pscales[:, pc * PW:(pc + 1) * PW],
                                 start=start, stop=stop)
 
         def first(g, pc):
-            x = psum.tile([P, 512], F32, name="aux", bufs=4)
+            x = psum.tile([P, PW], F32, name="aux", bufs=4)
             fp_pass(x, 2 * g, 0, pc)
-            rmax[g][pc] = work.tile([P, 512], F32, name="rmax%d" % pc, bufs=3)
+            rmax[g][pc] = work.tile([P, PW], F32, name="rmax%d" % pc, bufs=3)
             nc.scalar.activation(out=rmax[g][pc][:], in_=x[:], func=ACT.Identity,
                                  bias=ng_sb[2 * g][:, 0:1], scale=1.0)
 
-        def pair(m, jl, pc, sums):
-            i = negated(m).index(jl + 1)
-            xd = psum.tile([P, 512], F32, name="aux", bufs=4)
-            fp_pass(xd, m, jl, pc, start=True, stop=False)
-            fp_pass(xd, m, 4 + i, pc, start=False, stop=True)
-            dd = work.tile([P, 512], F32, name="dd", bufs=4)
-            nc.scalar.activation(out=dd[:], in_=xd[:], func=ACT.Relu, bias=dng_sb[m][i][:], scale=1.0)
-            xb = psum.tile([P, 512], F32, name="aux", bufs=4)
-            fp_pass(xb, m, jl + 1, pc)
-            nc.scalar.activation(out=sums[:], in_=xb[:], func=ACT.Identity,
-                                 bias=ng_sb[m][:, jl + 1:jl + 2], scale=1.0)
-            nc.gpsimd.tensor_tensor(out=sums[:], in0=sums[:], in1=dd[:], op=ALU.add)
-
-        joined = {}
-
-        def late_pair(jl, pc):
-            joined[jl, pc] = work.tile([P, 512], F32, name="joined", bufs=8)
-            pair(NCHUNK - 1, jl, pc, joined[jl, pc])
-
-        def merge(jl, pc):
-            r = rmax[NG - 1][pc]
-            nc.vector.tensor_tensor(out=r[:], in0=r[:], in1=joined[jl, pc][:], op=ALU.max)
-
         def tile2(g, j, pc):
-            m = 2 * g + j // 4
-            jl = j % 4
-            x = psum.tile([P, 512], F32, name="x", bufs=4)
+            m = 2 * g + j // TC
+            jl = j % TC
+            x = psum.tile([P, PW], F32, name="x", bufs=4)
             fp_pass(x, m, jl, pc)
             nc.vector.scalar_tensor_tensor(out=rmax[g][pc][:], in0=x[:], scalar=ng_sb[m][:, jl:jl + 1],
                                            in1=rmax[g][pc][:], op0=ALU.add, op1=ALU.max)
@@ -259,41 +242,55 @@ def tile_protopnet_pa_kernel(tc, h_relu, conv2_w, conv2_b, prototypes, out):
             bank = psum.tile([P, 4, P], F32, name="x", bufs=4)
             for a in range(4):
                 nc.tensor.transpose(bank[:, a, :], rmax[g][pc][:, a * P:(a + 1) * P], ident[:])
-            bview = best[:].rearrange("p (b t) -> p t b", t=16)
+            bview = best[:].rearrange("p (b t) -> p t b", t=NPT)
             nc.vector.tensor_reduce(out=bview[:, 4 * pc:4 * pc + 4, GI * g:GI * (g + 1)],
                                     in_=bank[:].rearrange("p a (i r) -> p a i r", i=GI),
                                     axis=AX.X, op=ALU.max)
 
-        wb = words_transpose(w_sb, 0)
-        wg = words_copy(wb, "s")
-        hreg(0, "v", [0, 1])
-        hreg(0, "v", [2, 3])
-        words_quant(wg, wcodes[:], wscales[:])
-        quant_h(0)
-        pb = words_transpose(proto_sb, 0)
-        pg0 = words_copy(pb, "s")
-        hreg(1, "v")
-        pb = words_transpose(proto_sb, 4)
-        pg1 = words_copy(pb, "v")
-        for t in range(4):
-            st1(0, t)
-        quant_h(1)
-        words_quant(pg0, *proto_cols(0))
-        words_quant(pg1, *proto_cols(1))
-        pb = words_transpose(proto_sb, 8)
-        pg2 = words_copy(pb, "v")
-        fint(0, "v")
-        words_quant(pg2, *proto_cols(2))
-        quant_f(0)
-        for jl in range(4):
-            f2_tile(0, jl)
-        pb = words_transpose(proto_sb, 12)
-        pg3 = words_copy(pb, "v", gp_tile())
-        first(0, 0)
-        first(0, 1)
-        first(0, 2)
-        words_quant(pg3, *proto_cols(3))
-        hreg(2, "g")
+        def terms(jl, pc, dd, bb):
+            m = LAST_CHUNK
+            i = negated(m).index(jl + 1)
+            xd = psum.tile([P, PW], F32, name="aux", bufs=4)
+            fp_pass(xd, m, jl, pc, start=True, stop=False)
+            fp_pass(xd, m, TC + i, pc, start=False, stop=True)
+            nc.scalar.activation(out=dd[:], in_=xd[:], func=ACT.Relu, bias=dng_sb[m][i][:], scale=1.0)
+            xb = psum.tile([P, PW], F32, name="aux", bufs=4)
+            fp_pass(xb, m, jl + 1, pc)
+            nc.scalar.activation(out=bb[:], in_=xb[:], func=ACT.Identity,
+                                 bias=ng_sb[m][:, jl + 1:jl + 2], scale=1.0)
+
+        joined = {}
+        apart = {}
+
+        def joined_pair(pc):
+            dd = work.tile([P, PW], F32, name="dd", bufs=4)
+            joined[pc] = work.tile([P, PW], F32, name="joined", bufs=4)
+            terms(0, pc, dd, joined[pc])
+            nc.gpsimd.tensor_tensor(out=joined[pc][:], in0=joined[pc][:], in1=dd[:], op=ALU.add)
+
+        def merge(pc):
+            r = rmax[LAST][pc]
+            nc.vector.tensor_tensor(out=r[:], in0=r[:], in1=joined[pc][:], op=ALU.max)
+
+        def apart_pair(pc):
+            dd = work.tile([P, PW], F32, name="apart_d", bufs=4)
+            bb = work.tile([P, PW], F32, name="apart_b", bufs=4)
+            terms(2, pc, dd, bb)
+            apart[pc] = (bb, dd)
+
+        def fold_sum(pc):
+            bank = psum.tile([P, 4, P], F32, name="x", bufs=4)
+            bb, dd = apart[pc]
+            for a in range(4):
+                cols = slice(a * P, (a + 1) * P)
+                nc.tensor.matmul(out=bank[:, a, :], lhsT=bb[:, cols], rhs=ident[:], start=True, stop=False,
+                                 is_transpose=True)
+                nc.tensor.matmul(out=bank[:, a, :], lhsT=dd[:, cols], rhs=ident[:], start=False, stop=True,
+                                 is_transpose=True)
+            bview = best67[:].rearrange("p (i t) -> p t i", t=NPT)
+            nc.vector.tensor_reduce(out=bview[:, 4 * pc:4 * pc + 4, :],
+                                    in_=bank[:].rearrange("p a (i r) -> p a i r", i=GI),
+                                    axis=AX.X, op=ALU.max)
 
         p2_next = [0]
 
@@ -303,94 +300,123 @@ def tile_protopnet_pa_kernel(tc, h_relu, conv2_w, conv2_b, prototypes, out):
             nc.scalar.activation(out=junk[:], in_=proto_sb[:, rt, :], func=ACT.Square,
                                  accum_out=p2_sb[:, rt:rt + 1])
 
-        def at(plan, places, work_of):
-            for k, place in enumerate(places):
-                plan[place].append(lambda k=k: work_of(k))
+        words = words_transpose(w_sb, 0)
+        wg = words_copy(words, "s")
+        for i in range(GI):
+            hreg(0, "v", [i])
+            if i == 0:
+                hreg(1, "v", [0])
+        hreg(1, "s", [1, 2])
+        words_quant(wg, wcodes[:], wscales[:])
+        quant_h(0)
+        words = words_transpose(proto_sb, 0)
+        pg0 = words_copy(words, "s")
+        words = words_transpose(proto_sb, 4)
+        for t in range(4):
+            st1(0, t)
+        hreg(1, "v", [3])
+        quant_h(1)
+        pg1 = words_copy(words, "v", halves=[0])
+        words_quant(pg0, *proto_cols(0))
+        words_copy(words, "v", pg1, halves=[1])
+        words = words_transpose(proto_sb, 8)
+        words_quant(pg1, *proto_cols(1))
+        pg2 = words_copy(words, "v")
+        fint(0, "v")
+        words_quant(pg2, *proto_cols(2))
+        for jl in range(TC):
+            f2_tile(0, jl)
+        words = words_transpose(proto_sb, 12)
+        quant_f(0)
+        pg3 = words_copy(words, "v", gp_tile())
+        for pc in range(NPC - 1):
+            first(0, pc)
+        words_quant(pg3, *proto_cols(3))
+        hreg(2, "g")
 
-        last = NG - 1
-        pairs = [(0, 0), (0, 1), (0, 2), (0, 3), (2, 3), (2, 2), (2, 1), (2, 0)][:4]
-        for g in range(NG - 1):
-            plan = [[] for k in range(28)]
+        places = [
+            dict(first0=[1], fold=[], st_odd=[1, 1, 2, 3], q_e=[4], f2_odd=[7, 7, 9, 9], qf_odd=[10],
+                 st_e=[11, 11, 13, 13], qh_o=[16], f2_e=[16, 16, 18, 18], st_o=[20, 20, 22, 22], qf_e=[22], qh_next=[],
+                 first=[25, 26, 27, 27], f2_o=[], p2=[], qf_o=[]),
+            dict(first0=[], fold=[1, 3, 9, 11], st_odd=[], q_e=[0], f2_odd=[1, 1, 3, 3], qf_odd=[5],
+                 st_e=[5, 5, 7, 7], qh_o=[11], f2_e=[9, 9, 11, 11], st_o=[14, 14, 16, 16], qf_e=[17], qh_next=[23],
+                 first=[21, 23, 25, 27], f2_o=[], p2=[16, 17, 18, 19, 20, 21, 22, 23], qf_o=[]),
+            dict(first0=[], fold=[1, 3, 9, 11], st_odd=[], q_e=[], f2_odd=[1, 1, 3, 3], qf_odd=[3],
+                 st_e=[5, 5, 7, 7], qh_o=[10], f2_e=[9, 9, 11, 11], st_o=[13, 13, 15, 15], qf_e=[16], qh_next=[],
+                 first=[21, 23, 25, 27], f2_o=[18, 18, 20, 20], p2=[24, 25, 26, 27], qf_o=[25]),
+        ]
+        turns = [(j, pc) for j in range(1, NJ) for pc in range(NPC)]
+        for g in range(LAST):
             odd = 2 * g + 1
             e = odd + 1
             o = odd + 2
-            late = 0
-            if g == 0:
-                qf_odd, qh_o, qf_e, qh_ne = 9, 14, 19, 26
-                plan[0].append(lambda: first(0, 3))
-                at(plan, [0, 1, 2, 3], lambda k: st1(1, k))
-                at(plan, [16, 17, 18, 19, 20], lambda k: p2_part())
-                plan[4].append(lambda: quant_h(2))
-                plan[4].append(lambda: fint(1, "g"))
-            elif g == 1:
-                qf_odd, qh_o, qf_e, qh_ne = 3, 10, 16, 22
-                at(plan, [16, 17, 18, 19, 20, 22, 24, 26], lambda k: p2_part())
-            else:
-                qf_odd, qh_o, qf_e, qf_o = 3, 10, 16, 25
-            if g > 0:
-                at(plan, [1, 3, 9, 11] if g == 1 else [1, 3, 9, 11], lambda k: fold(g - 1, k))
-            at(plan, [5, 5, 7, 7] if g == 0 else [1, 1, 3, 3], lambda k: f2_tile(odd, k))
-            plan[qf_odd].append(lambda: quant_f(odd))
-            plan[qf_odd].append(lambda: hreg(o, "g"))
-            at(plan, [9, 9, 11, 11] if g == 0 else [5, 5, 7, 7], lambda k: st1(e, k))
-            plan[qh_o].append(lambda: quant_h(o))
-            plan[qh_o].append(lambda: fint(e, "g"))
-            at(plan, [13, 13, 15, 15] if g == 0 else [9, 9, 11, 11], lambda k: f2_tile(e, k))
-            plan[qf_e].append(lambda: quant_f(e))
-            if g + 2 < NG:
-                plan[qf_e].append(lambda: hreg(e + 2, "g"))
-                plan[qh_ne].append(lambda: quant_h(e + 2))
-                at(plan, [21, 23, 25, 27] if g == 0 else [21, 23, 25, 27], lambda k: first(g + 1, k))
-                at(plan, [17, 17, 19, 19] if g == 0 else [13, 13, 15, 15], lambda k: st1(o, k))
-                plan[qh_ne].append(lambda: fint(o, "g"))
-            else:
-                at(plan, [13, 13, 15, 15], lambda k: st1(o, k))
-                plan[qf_e].append(lambda: fint(o, "g"))
-                at(plan, [18, 18, 20, 20], lambda k: f2_tile(o, k))
-                at(plan, [20, 22, 24], lambda k: p2_part())
-                plan[qf_o].append(lambda: quant_f(o))
-                at(plan, [21, 23, 25, 27], lambda k: first(g + 1, k))
-                at(plan, [], lambda k: late_pair(*pairs[k]))
-            for k in range(28):
-                tile2(g, 1 + k // 4, k % 4)
-                for f in plan[k]:
-                    f()
+            plan = [[] for turn in turns]
 
-        units = [lambda pc=pc: tile2(last, 1, pc) for pc in range(NPC)]
-        units += [lambda pc=pc: tile2(last, 2, pc) for pc in range(NPC)]
-        units += [lambda pc=pc: fold(last - 1, pc) for pc in range(NPC)]
-        units += [lambda pc=pc: tile2(last, 3, pc) for pc in range(NPC)]
-        ends = []
-        for half in ((0, 1), (2, 3)):
-            alone = [pc for pc in half if (2, pc) not in pairs]
-            ends += [lambda j=j, pc=pc: tile2(last, j, pc) for j in (6, 7) for pc in alone]
-            ends += [lambda jl=jl, pc=pc: merge(jl, pc) for jl in (0, 2) for pc in half if (jl, pc) in pairs]
-            if half == (0, 1):
-                first_half = len(ends)
-        ends.insert(first_half + 1, lambda: fold(last, 0))
-        ends.insert(first_half + 3, lambda: fold(last, 1))
-        done = 0
-        for k, unit in enumerate(units + ends[:4]):
+            def put(name, work_of):
+                for k, place in enumerate(places[g][name]):
+                    plan[place].append(lambda k=k: work_of(k))
+
+            put("first0", lambda k: first(0, NPC - 1))
+            put("fold", lambda k: fold(g - 1, k))
+            put("st_odd", lambda k: st1(odd, k))
+            put("q_e", lambda k: quant_h(e))
+            put("q_e", lambda k: fint(odd, "g"))
+            put("f2_odd", lambda k: f2_tile(odd, k))
+            put("qf_odd", lambda k: quant_f(odd))
+            put("qf_odd", lambda k: hreg(o, "g"))
+            put("st_e", lambda k: st1(e, k))
+            put("qh_o", lambda k: quant_h(o))
+            put("qh_o", lambda k: fint(e, "g"))
+            put("f2_e", lambda k: f2_tile(e, k))
+            put("qf_e", lambda k: quant_f(e))
+            if o < LAST_CHUNK:
+                put("qf_e", lambda k: hreg(o + 1, "g"))
+            put("qh_next", lambda k: quant_h(o + 1))
+            put("first", lambda k: first(g + 1, k))
+            put("st_o", lambda k: st1(o, k))
+            put("qh_next", lambda k: fint(o, "g"))
+            if o == LAST_CHUNK:
+                put("qf_e", lambda k: fint(o, "g"))
+            put("f2_o", lambda k: f2_tile(o, k))
+            put("p2", lambda k: p2_part())
+            put("qf_o", lambda k: quant_f(o))
+            for k, (j, pc) in enumerate(turns):
+                tile2(g, j, pc)
+                for step in plan[k]:
+                    step()
+
+        units = [lambda j=j, pc=pc: tile2(LAST, j, pc) for j in (1, 2) for pc in range(NPC)]
+        units += [lambda pc=pc: fold(LAST - 1, pc) for pc in range(NPC)]
+        units += [lambda pc=pc: tile2(LAST, 3, pc) for pc in range(NPC)]
+        units += [lambda j=j, pc=pc: tile2(LAST, j, pc) for j in (6, 7) for pc in range(NPC) if pc not in APART_COLS]
+        pairs = [lambda pc=pc: joined_pair(pc) for pc in range(NPC)]
+        pairs += [lambda pc=pc: apart_pair(pc) for pc in APART_COLS]
+        for k, unit in enumerate(units):
             unit()
-            if k >= 1 and (k - 1) % 4 == 0 and done < len(pairs):
-                late_pair(*pairs[done])
-                done += 1
-        for k in range(done, len(pairs)):
-            late_pair(*pairs[k])
-        for k in range(16 - p2_next[0]):
+            if k % 4 == 0:
+                pairs[k // 4]()
+        pairs[len(pairs) - 1]()
+        for k in range(NPT - p2_next[0]):
             p2_part()
-        for end in ends[4:]:
-            end()
-        fold(last, 2)
-        fold(last, 3)
+        for half in range(2):
+            cols = (2 * half, 2 * half + 1)
+            for pc in cols:
+                merge(pc)
+            fold_sum(APART_COLS[half])
+            for pc in cols:
+                fold(LAST, pc)
+        t0 = 4 * APART_COLS[0]
+        tail = best[:, GI * NPT * LAST:].rearrange("p (i t) -> p i t", t=NPT)[:, :, t0:]
+        tail67 = best67[:].rearrange("p (i t) -> p i t", t=NPT)[:, :, t0:]
+        nc.vector.tensor_tensor(out=tail, in0=tail, in1=tail67, op=ALU.max)
 
         for half in range(2):
             res = const.tile([P, P], F32, name="res%d" % half)
             nc.vector.scalar_tensor_tensor(
-                out=res[:].rearrange("p (b t) -> p b t", t=16),
-                in0=best[:, half * P:(half + 1) * P].rearrange("p (b t) -> p b t", t=16),
+                out=res[:].rearrange("p (b t) -> p b t", t=NPT),
+                in0=best[:, half * P:(half + 1) * P].rearrange("p (b t) -> p b t", t=NPT),
                 scalar=-2.0,
-                in1=p2_sb[:].unsqueeze(1).to_broadcast([P, 8, 16]),
+                in1=p2_sb[:].unsqueeze(1).to_broadcast([P, 8, NPT]),
                 op0=ALU.mult, op1=ALU.add)
             tpf = psum.tile([P, P], F32, name="aux", bufs=4)
             nc.tensor.transpose(tpf[:], res[:], ident[:])

from contextlib import ExitStack

import concourse.mybir as mybir
from concourse.masks import make_identity

F32 = mybir.dt.float32
BF16 = mybir.dt.bfloat16
U32 = mybir.dt.uint32
U8 = mybir.dt.uint8
FP8X4 = mybir.dt.float8_e4m3fn_x4
ACT = mybir.ActivationFunctionType
ALU = mybir.AluOpType
AX = mybir.AxisListType

P = 128
NIMG = 16
HW = 256
CH = 512
NPROTO = 2048
GI = 4
NG = NIMG // GI
RPOS = P // GI
NJ = HW // RPOS
CW = 512
TC = CW // P
NCHUNK = NIMG * HW // CW
PW = 512
NPC = NPROTO // PW
NPT = NPROTO // P
LAST = NG - 1
LAST_CHUNK = NCHUNK - 1

APART_COLS = (2, 3)

FLOPS = 2 * CH * CH * NIMG * HW + 2 * NPROTO * CH * NIMG * HW


def tile_protopnet_pa_kernel(tc, h_relu, conv2_w, conv2_b, prototypes, out):
    nc = tc.nc
    with ExitStack() as ctx:
        ctx.enter_context(tc.manual_schedule())
        const = ctx.enter_context(tc.tile_pool(name="const", bufs=1))
        work = ctx.enter_context(tc.tile_pool(name="work", bufs=2))
        psum = ctx.enter_context(tc.psum_pool(name="psum", bufs=2))

        w_sb = const.tile([P, 4, CH], BF16)
        nc.sync.dma_start(out=w_sb[:], in_=conv2_w.rearrange("(q t) c -> q t c", t=4))
        b_bf = const.tile([P, 4], BF16)
        nc.scalar.dma_start(out=b_bf[:], in_=conv2_b.rearrange("(q t) -> q t", t=4))
        h_sb = [None] * NG
        proto_sb = const.tile([P, NPT, CH], BF16)

        def load_h(g, pieces):
            h_sb[g] = work.tile([P, GI, 4 * HW], BF16, name="h_sb", bufs=NG)
            n = GI // pieces
            for k in range(pieces):
                nc.sync.dma_start(
                    out=h_sb[g][:, k * n:(k + 1) * n],
                    in_=h_relu[g * GI + k * n:g * GI + (k + 1) * n].rearrange("i (p j) y x -> p i (j y x)", j=4),
                )

        def load_proto(pc):
            nc.sync.dma_start(
                out=proto_sb[:, 4 * pc:4 * pc + 4, :],
                in_=prototypes[pc * PW:(pc + 1) * PW, :].rearrange("(a r) d -> r a d", r=P),
            )

        load_h(0, GI)
        for pc in range(NPC):
            load_proto(pc)
        for g in range(1, NG):
            load_h(g, 1)

        ident = const.tile([P, P], F32)
        make_identity(nc, ident[:])
        b_f32 = const.tile([P, 4], F32)
        nc.vector.tensor_copy(out=b_f32[:], in_=b_bf[:])

        wcodes = const.tile([P, CH], U32, align_bytes=64)
        wscales = const.tile([P, CH], U8, align_bytes=64)
        pcodes = const.tile([P, NPROTO], U32, align_bytes=64)
        pscales = const.tile([P, NPROTO], U8, align_bytes=64)
        p2_sb = const.tile([P, NPT], F32)
        junk = const.tile([P, CH], BF16)
        junk32 = const.tile([P, CH], BF16)
        best = const.tile([P, NIMG * NPT], F32)
        best67 = const.tile([P, GI * NPT], F32)

        def words_transpose(src, first_tile):
            banks = []
            for half in range(2):
                bank = psum.tile([P, 2, 2, P], F32, name="x", bufs=4)
                for a in range(2):
                    words = src[:, first_tile + 2 * half + a, :].bitcast(F32)
                    words = words.rearrange("r (q u) -> r u q", u=2)
                    for u in range(2):
                        nc.tensor.transpose(bank[:, a, u, :], words[:, u, :], ident[:])
                banks.append(bank)
            return banks

        def words_copy(banks, eng, grouped=None, halves=(0, 1)):
            if grouped is None:
                grouped = work.tile([P, 4 * PW], BF16, name="grouped", align_bytes=64)
            gw = grouped[:, :4 * PW].bitcast(F32)
            for half in halves:
                dst = gw[:, half * 512:(half + 1) * 512].rearrange("q (a r u) -> q a r u", a=2, u=2)
                src = banks[half][:].rearrange("q a u r -> q a r u")
                if eng == "v":
                    nc.vector.tensor_copy(out=dst, in_=src)
                else:
                    nc.scalar.copy(out=dst, in_=src)
            return grouped

        def words_quant(grouped, codes, scales):
            nc.vector.quantize_mx(out=codes.bitcast(FP8X4), scales=scales, in_=grouped[:, :4 * PW])

        def proto_cols(pc):
            return pcodes[:, pc * PW:(pc + 1) * PW], pscales[:, pc * PW:(pc + 1) * PW]

        hg = [None] * NCHUNK
        hcodes = [None] * NCHUNK
        hscales = [None] * NCHUNK
        f32c = [None] * NCHUNK
        f2c = [None] * NCHUNK
        fgc = [None] * NCHUNK
        fcodes = [None] * NCHUNK
        fscales = [None] * NCHUNK
        ng_sb = [None] * NCHUNK
        dng_sb = [[] for m in range(NCHUNK)]
        rmax = [[None] * NPC for g in range(NG)]

        def gp_tile():
            return work.tile([P, 6 * CW], BF16, name="gp_out", bufs=1, align_bytes=64)

        def hreg(m, eng, images=range(GI)):
            g = m // 2
            j0 = TC * (m % 2)
            if hg[m] is None:
                if eng == "g":
                    hg[m] = gp_tile()
                else:
                    hg[m] = work.tile([P, 4 * CW], BF16, name="hg%d" % m, bufs=1, align_bytes=64)
            dst = hg[m][:, :4 * CW].rearrange("p (j i r c) -> p i j r c", j=TC, i=GI, c=4)
            src = h_sb[g][:].rearrange("p i (c j r) -> p i j r c", c=4, j=NJ)[:, :, j0:j0 + TC]
            if eng == "g":
                nc.gpsimd.tensor_scalar(out=dst, in0=src, scalar1=1.0, scalar2=0.0, op0=ALU.mult, op1=ALU.add)
            else:
                for i in images:
                    if eng == "v":
                        nc.vector.tensor_copy(out=dst[:, i], in_=src[:, i])
                    else:
                        nc.scalar.copy(out=dst[:, i], in_=src[:, i])

        def quant_h(m):
            hcodes[m] = work.tile([P, CW], U32, name="hcodes", bufs=4, align_bytes=64)
            hscales[m] = work.tile([P, CW], U8, name="hscales", bufs=4, align_bytes=64)
            nc.vector.quantize_mx(out=hcodes[m][:].bitcast(FP8X4), scales=hscales[m][:], in_=hg[m][:, :4 * CW])

        def st1(m, t):
            if t == 0:
                f32c[m] = work.tile([P, 4, CW], F32, name="f32c", bufs=3)
            z = psum.tile([P, CW], F32, name="aux", bufs=4)
            nc.tensor.matmul_mx(out=z[:], lhsT=wcodes[:, t * P:(t + 1) * P].bitcast(FP8X4),
                                lhsT_scale=wscales[:, t * P:(t + 1) * P],
                                rhs=hcodes[m][:].bitcast(FP8X4), rhs_scale=hscales[m][:],
                                start=True, stop=True)
            nc.scalar.activation(out=f32c[m][:, t, :], in_=z[:], func=ACT.Sigmoid,
                                 bias=b_f32[:, t:t + 1], scale=1.0)

        def negated(m):
            return [1, 3] if m == LAST_CHUNK else []

        def f2_tile(m, jl):
            if jl == 0:
                f2c[m] = work.tile([P, TC], F32, name="f2c", bufs=4)
            bank = psum.tile([P, 4, P], F32, name="aux", bufs=4)
            for t in range(4):
                nc.tensor.transpose(bank[:, t, :], f32c[m][:, t, jl * P:(jl + 1) * P], ident[:])
            nc.scalar.activation(out=junk32[:], in_=bank[:].rearrange("p t q -> p (t q)"), func=ACT.Square,
                                 accum_out=f2c[m][:, jl:jl + 1])
            if jl == TC - 1:
                ng_sb[m] = work.tile([P, TC], F32, name="ng_sb", bufs=4)
                nc.scalar.mul(out=ng_sb[m][:], in_=f2c[m][:], mul=-0.5)
                for i, jn in enumerate(negated(m)):
                    dng_sb[m].append(work.tile([P, 1], F32, name="dng_sb", bufs=3))
                    nc.scalar.activation(out=dng_sb[m][i][:], in_=f2c[m][:, jn:jn + 1], func=ACT.Identity,
                                         bias=ng_sb[m][:, jn - 1:jn], scale=0.5)

        def fint(m, eng):
            if eng == "v":
                fgc[m] = work.tile([P, 4 * CW], BF16, name="fg_v", bufs=1, align_bytes=64)
            else:
                fgc[m] = gp_tile()
            dst = fgc[m][:, :4 * CW].rearrange("p (c t) -> p c t", t=4)
            src = f32c[m][:].rearrange("p t c -> p c t")
            if eng == "v":
                nc.vector.tensor_copy(out=dst, in_=src)
            else:
                for i, jn in enumerate(negated(m)):
                    nc.gpsimd.tensor_scalar(
                        out=fgc[m][:, (4 + i) * CW:(5 + i) * CW].rearrange("p (c t) -> p c t", t=4),
                        in0=f32c[m][:, :, jn * P:(jn + 1) * P].rearrange("p t c -> p c t"),
                        scalar1=-1.0, scalar2=0.0, op0=ALU.mult, op1=ALU.add)
                nc.gpsimd.tensor_scalar(out=dst, in0=src, scalar1=1.0, scalar2=0.0,
                                        op0=ALU.mult, op1=ALU.add)

        def quant_f(m):
            width = CW + 2 * P
            fcodes[m] = work.tile([P, width], U32, name="fcodes", bufs=4, align_bytes=64)
            fscales[m] = work.tile([P, width], U8, name="fscales", bufs=4, align_bytes=64)
            nc.vector.quantize_mx(out=fcodes[m][:, :CW].bitcast(FP8X4), scales=fscales[m][:, :CW],
                                  in_=fgc[m][:, :4 * CW])
            n = len(negated(m))
            if n > 0:
                nc.vector.quantize_mx(out=fcodes[m][:, CW:CW + n * P].bitcast(FP8X4),
                                      scales=fscales[m][:, CW:CW + n * P],
                                      in_=fgc[m][:, 4 * CW:(4 + n) * CW])

        def fp_pass(x, m, jl, pc, start=True, stop=True):
            nc.tensor.matmul_mx(out=x[:], lhsT=fcodes[m][:, jl * P:(jl + 1) * P].bitcast(FP8X4),
                                lhsT_scale=fscales[m][:, jl * P:(jl + 1) * P],
                                rhs=pcodes[:, pc * PW:(pc + 1) * PW].bitcast(FP8X4),
                                rhs_scale=pscales[:, pc * PW:(pc + 1) * PW],
                                start=start, stop=stop)

        def first(g, pc):
            x = psum.tile([P, PW], F32, name="aux", bufs=4)
            fp_pass(x, 2 * g, 0, pc)
            rmax[g][pc] = work.tile([P, PW], F32, name="rmax%d" % pc, bufs=3)
            nc.scalar.activation(out=rmax[g][pc][:], in_=x[:], func=ACT.Identity,
                                 bias=ng_sb[2 * g][:, 0:1], scale=1.0)

        def tile2(g, j, pc):
            m = 2 * g + j // TC
            jl = j % TC
            x = psum.tile([P, PW], F32, name="x", bufs=4)
            fp_pass(x, m, jl, pc)
            nc.vector.scalar_tensor_tensor(out=rmax[g][pc][:], in0=x[:], scalar=ng_sb[m][:, jl:jl + 1],
                                           in1=rmax[g][pc][:], op0=ALU.add, op1=ALU.max)

        def fold(g, pc):
            bank = psum.tile([P, 4, P], F32, name="x", bufs=4)
            for a in range(4):
                nc.tensor.transpose(bank[:, a, :], rmax[g][pc][:, a * P:(a + 1) * P], ident[:])
            bview = best[:].rearrange("p (b t) -> p t b", t=NPT)
            nc.vector.tensor_reduce(out=bview[:, 4 * pc:4 * pc + 4, GI * g:GI * (g + 1)],
                                    in_=bank[:].rearrange("p a (i r) -> p a i r", i=GI),
                                    axis=AX.X, op=ALU.max)

        def terms(jl, pc, dd, bb):
            m = LAST_CHUNK
            i = negated(m).index(jl + 1)
            xd = psum.tile([P, PW], F32, name="aux", bufs=4)
            fp_pass(xd, m, jl, pc, start=True, stop=False)
            fp_pass(xd, m, TC + i, pc, start=False, stop=True)
            nc.scalar.activation(out=dd[:], in_=xd[:], func=ACT.Relu, bias=dng_sb[m][i][:], scale=1.0)
            xb = psum.tile([P, PW], F32, name="aux", bufs=4)
            fp_pass(xb, m, jl + 1, pc)
            nc.scalar.activation(out=bb[:], in_=xb[:], func=ACT.Identity,
                                 bias=ng_sb[m][:, jl + 1:jl + 2], scale=1.0)

        joined = {}
        apart = {}

        def joined_pair(pc):
            dd = work.tile([P, PW], F32, name="dd", bufs=4)
            joined[pc] = work.tile([P, PW], F32, name="joined", bufs=4)
            terms(0, pc, dd, joined[pc])
            nc.gpsimd.tensor_tensor(out=joined[pc][:], in0=joined[pc][:], in1=dd[:], op=ALU.add)

        def merge(pc):
            r = rmax[LAST][pc]
            nc.vector.tensor_tensor(out=r[:], in0=r[:], in1=joined[pc][:], op=ALU.max)

        def apart_pair(pc):
            dd = work.tile([P, PW], F32, name="apart_d", bufs=4)
            bb = work.tile([P, PW], F32, name="apart_b", bufs=4)
            terms(2, pc, dd, bb)
            apart[pc] = (bb, dd)

        def fold_sum(pc):
            bank = psum.tile([P, 4, P], F32, name="x", bufs=4)
            bb, dd = apart[pc]
            for a in range(4):
                cols = slice(a * P, (a + 1) * P)
                nc.tensor.matmul(out=bank[:, a, :], lhsT=bb[:, cols], rhs=ident[:], start=True, stop=False,
                                 is_transpose=True)
                nc.tensor.matmul(out=bank[:, a, :], lhsT=dd[:, cols], rhs=ident[:], start=False, stop=True,
                                 is_transpose=True)
            bview = best67[:].rearrange("p (i t) -> p t i", t=NPT)
            nc.vector.tensor_reduce(out=bview[:, 4 * pc:4 * pc + 4, :],
                                    in_=bank[:].rearrange("p a (i r) -> p a i r", i=GI),
                                    axis=AX.X, op=ALU.max)

        p2_next = [0]

        def p2_part():
            rt = p2_next[0]
            p2_next[0] = rt + 1
            nc.scalar.activation(out=junk[:], in_=proto_sb[:, rt, :], func=ACT.Square,
                                 accum_out=p2_sb[:, rt:rt + 1])

        words = words_transpose(w_sb, 0)
        wg = words_copy(words, "s")
        for i in range(GI):
            hreg(0, "v", [i])
            if i == 0:
                hreg(1, "v", [0])
        hreg(1, "s", [1, 2])
        words_quant(wg, wcodes[:], wscales[:])
        quant_h(0)
        words = words_transpose(proto_sb, 0)
        pg0 = words_copy(words, "s")
        words = words_transpose(proto_sb, 4)
        for t in range(4):
            st1(0, t)
        hreg(1, "v", [3])
        quant_h(1)
        pg1 = words_copy(words, "v", halves=[0])
        words_quant(pg0, *proto_cols(0))
        words_copy(words, "v", pg1, halves=[1])
        words = words_transpose(proto_sb, 8)
        words_quant(pg1, *proto_cols(1))
        pg2 = words_copy(words, "v")
        fint(0, "v")
        words_quant(pg2, *proto_cols(2))
        for jl in range(TC):
            f2_tile(0, jl)
        words = words_transpose(proto_sb, 12)
        quant_f(0)
        pg3 = words_copy(words, "v", gp_tile())
        for pc in range(NPC - 1):
            first(0, pc)
        words_quant(pg3, *proto_cols(3))
        hreg(2, "g")

        places = [
            dict(first0=[1], fold=[], st_odd=[1, 1, 2, 3], q_e=[4], f2_odd=[7, 7, 9, 9], qf_odd=[10],
                 st_e=[11, 11, 13, 13], qh_o=[16], f2_e=[16, 16, 18, 18], st_o=[20, 20, 22, 22], qf_e=[22], qh_next=[],
                 first=[25, 26, 27, 27], f2_o=[], p2=[], qf_o=[]),
            dict(first0=[], fold=[1, 3, 9, 11], st_odd=[], q_e=[0], f2_odd=[1, 1, 3, 3], qf_odd=[5],
                 st_e=[5, 5, 7, 7], qh_o=[11], f2_e=[9, 9, 11, 11], st_o=[14, 14, 16, 16], qf_e=[17], qh_next=[23],
                 first=[21, 23, 25, 27], f2_o=[], p2=[16, 17, 18, 19, 20, 21, 22, 23], qf_o=[]),
            dict(first0=[], fold=[1, 3, 9, 11], st_odd=[], q_e=[], f2_odd=[1, 1, 3, 3], qf_odd=[3],
                 st_e=[5, 5, 7, 7], qh_o=[10], f2_e=[9, 9, 11, 11], st_o=[13, 13, 15, 15], qf_e=[16], qh_next=[],
                 first=[21, 23, 25, 27], f2_o=[18, 18, 20, 20], p2=[24, 25, 26, 27], qf_o=[25]),
        ]
        turns = [(j, pc) for j in range(1, NJ) for pc in range(NPC)]
        for g in range(LAST):
            odd = 2 * g + 1
            e = odd + 1
            o = odd + 2
            plan = [[] for turn in turns]

            def put(name, work_of):
                for k, place in enumerate(places[g][name]):
                    plan[place].append(lambda k=k: work_of(k))

            put("first0", lambda k: first(0, NPC - 1))
            put("fold", lambda k: fold(g - 1, k))
            put("st_odd", lambda k: st1(odd, k))
            put("q_e", lambda k: quant_h(e))
            put("q_e", lambda k: fint(odd, "g"))
            put("f2_odd", lambda k: f2_tile(odd, k))
            put("qf_odd", lambda k: quant_f(odd))
            put("qf_odd", lambda k: hreg(o, "g"))
            put("st_e", lambda k: st1(e, k))
            put("qh_o", lambda k: quant_h(o))
            put("qh_o", lambda k: fint(e, "g"))
            put("f2_e", lambda k: f2_tile(e, k))
            put("qf_e", lambda k: quant_f(e))
            if o < LAST_CHUNK:
                put("qf_e", lambda k: hreg(o + 1, "g"))
            put("qh_next", lambda k: quant_h(o + 1))
            put("first", lambda k: first(g + 1, k))
            put("st_o", lambda k: st1(o, k))
            put("qh_next", lambda k: fint(o, "g"))
            if o == LAST_CHUNK:
                put("qf_e", lambda k: fint(o, "g"))
            put("f2_o", lambda k: f2_tile(o, k))
            put("p2", lambda k: p2_part())
            put("qf_o", lambda k: quant_f(o))
            for k, (j, pc) in enumerate(turns):
                tile2(g, j, pc)
                for step in plan[k]:
                    step()

        units = [lambda j=j, pc=pc: tile2(LAST, j, pc) for j in (1, 2) for pc in range(NPC)]
        units += [lambda pc=pc: fold(LAST - 1, pc) for pc in range(NPC)]
        units += [lambda pc=pc: tile2(LAST, 3, pc) for pc in range(NPC)]
        units += [lambda j=j, pc=pc: tile2(LAST, j, pc) for j in (6, 7) for pc in range(NPC) if pc not in APART_COLS]
        pairs = [lambda pc=pc: joined_pair(pc) for pc in range(NPC)]
        pairs += [lambda pc=pc: apart_pair(pc) for pc in APART_COLS]
        for k, unit in enumerate(units):
            unit()
            if k % 4 == 0:
                pairs[k // 4]()
        pairs[len(pairs) - 1]()
        for k in range(NPT - p2_next[0]):
            p2_part()
        for half in range(2):
            cols = (2 * half, 2 * half + 1)
            for pc in cols:
                merge(pc)
            fold_sum(APART_COLS[half])
            for pc in cols:
                fold(LAST, pc)
        t0 = 4 * APART_COLS[0]
        tail = best[:, GI * NPT * LAST:].rearrange("p (i t) -> p i t", t=NPT)[:, :, t0:]
        tail67 = best67[:].rearrange("p (i t) -> p i t", t=NPT)[:, :, t0:]
        nc.vector.tensor_tensor(out=tail, in0=tail, in1=tail67, op=ALU.max)

        for half in range(2):
            res = const.tile([P, P], F32, name="res%d" % half)
            nc.vector.scalar_tensor_tensor(
                out=res[:].rearrange("p (b t) -> p b t", t=NPT),
                in0=best[:, half * P:(half + 1) * P].rearrange("p (b t) -> p b t", t=NPT),
                scalar=-2.0,
                in1=p2_sb[:].unsqueeze(1).to_broadcast([P, 8, NPT]),
                op0=ALU.mult, op1=ALU.add)
            tpf = psum.tile([P, P], F32, name="aux", bufs=4)
            nc.tensor.transpose(tpf[:], res[:], ident[:])
            o_sb = const.tile([P, P], F32, name="o_sb%d" % half)
            nc.scalar.copy(out=o_sb[:], in_=tpf[:])
            nc.sync.dma_start(
                out=out.rearrange("b (t p) -> (b t) p", p=P)[half * P:(half + 1) * P, :],
                in_=o_sb[:])
